import numpy as np
import ml_dtypes


def mxq(x, axis, fmt="e4m3"):
    dtype, down = {"e4m3": (ml_dtypes.float8_e4m3fn, 7), "e5m2": (ml_dtypes.float8_e5m2, 14)}[fmt]
    v = np.moveaxis(np.asarray(x, np.float32).astype(ml_dtypes.bfloat16).astype(np.float64), axis, -1)
    blocks = v.reshape(v.shape[:-1] + (-1, 32))
    amax = np.abs(blocks).max(-1, keepdims=True)
    byte = np.maximum(np.where(amax > 0, np.frexp(amax)[1] - 1 + 127, 0) - down, 1)
    scale = np.exp2(byte - 127.0)
    codes = (blocks / scale).astype(np.float32).astype(dtype).astype(np.float64)
    return np.moveaxis((codes * scale).reshape(v.shape), -1, axis)


WIDE = False


def mx_kscale(k):
    if not WIDE:
        return np.ones(k)
    levels = np.array([10, -10, 5, -5, 0])
    a = np.random.permutation(np.resize(levels, k // 512 * 4)).reshape(k // 512, 4)
    idx = np.arange(k)
    return np.exp2(a[idx // 512, idx % 128 // 32])


BF16 = ml_dtypes.bfloat16


def bf(x):
    return np.asarray(x, np.float32).astype(BF16)


def f64(x):
    return np.asarray(x).astype(np.float64)


B, S, D, H, STRIDE = 1, 1024, 1024, 8, 32
DK = D // H


def strided_mask():
    i = np.arange(S)
    allowed = (i[:, None] == i[None, :]) | (np.minimum(i[:, None], i[None, :]) % STRIDE == 0)
    return np.where(allowed, 0.0, -np.inf)


def setup_inputs():
    t = mx_kscale(D)
    return {"qh": bf(np.random.standard_normal((B, H, S, DK))),
            "kh": bf(np.random.standard_normal((B, H, S, DK))),
            "vh": bf(np.random.standard_normal((B, H, S, DK)) * t.reshape(H, 1, DK)),
            "Wo": bf(np.random.standard_normal((D, D)) / np.sqrt(D) / t[:, None]),
            "bo": bf(np.random.standard_normal(D) * 0.1)}


def reference(qh, kh, vh, Wo, bo):
    s = f64(qh) @ f64(kh).transpose(0, 1, 3, 2) / np.sqrt(DK) + strided_mask()
    e = np.exp(s - s.max(-1, keepdims=True))
    ctx = (mxq(e, 3, "e4m3") @ mxq(f64(vh), 2, "e4m3")) / e.sum(-1, keepdims=True)
    ctx = ctx.transpose(0, 2, 1, 3).reshape(B, S, D)
    return (mxq(ctx, 2, "e4m3") @ mxq(f64(Wo), 0, "e4m3")) + f64(bo)

@@ -1,0 +1,411 @@
+from contextlib import ExitStack
+import math
+
+import concourse.mybir as mybir
+from concourse.masks import make_identity
+
+BF16 = mybir.dt.bfloat16
+F32 = mybir.dt.float32
+U32 = mybir.dt.uint32
+U8 = mybir.dt.uint8
+I32 = mybir.dt.int32
+FP8X4 = mybir.dt.float8_e4m3fn_x4
+ALU = mybir.AluOpType
+ACT = mybir.ActivationFunctionType
+AXIS_X = mybir.AxisListType.X
+
+P = 128
+H = 8
+S = 1024
+DK = 128
+D = H * DK
+NT = S // P
+NB = 32
+PACK = 4
+HG = 4
+N_HALF = 512
+SCALE = 1.0 / math.sqrt(DK)
+FILL_ON_SCALAR = 6
+NEG = -1.0e30
+
+FLOPS = 3 * 2 * S * S * D
+
+
+def quantise(nc, codes, scales, grouped):
+    nc.vector.quantize_mx(out=codes.bitcast(FP8X4), scales=scales, in_=grouped)
+
+
+def mx_pass(nc, acc, lhs, lhs_scale, rhs, rhs_scale, start, stop):
+    nc.tensor.matmul_mx(
+        out=acc,
+        lhsT=lhs.bitcast(FP8X4),
+        lhsT_scale=lhs_scale,
+        rhs=rhs.bitcast(FP8X4),
+        rhs_scale=rhs_scale,
+        start=start,
+        stop=stop,
+    )
+
+
+def tile_sparseattention_pa_kernel(tc, qh, kh, vh, Wo, bo, out):
+    nc = tc.nc
+    with ExitStack() as ctx:
+        const = ctx.enter_context(tc.tile_pool(name="const", bufs=1))
+        keep = ctx.enter_context(tc.tile_pool(name="keep", bufs=1))
+        loads = ctx.enter_context(tc.tile_pool(name="loads", bufs=3))
+        stage = ctx.enter_context(tc.tile_pool(name="stage", bufs=2))
+        psum_t = ctx.enter_context(tc.psum_pool(name="psum_t", bufs=3))
+        psum_f = ctx.enter_context(tc.psum_pool(name="psum_f", bufs=3))
+        psum_o = ctx.enter_context(tc.psum_pool(name="psum_o", bufs=2))
+
+        ident = const.tile([P, P], BF16)
+        make_identity(nc, ident[:])
+
+        mask_a32 = const.tile([P, NT, NB], F32)
+        nc.gpsimd.memset(mask_a32[:], 0.0)
+        nc.gpsimd.affine_select(
+            out=mask_a32[:],
+            in_=mask_a32[:],
+            pattern=[[1, NT], [-NB, NB]],
+            compare_op=ALU.is_ge,
+            fill=NEG,
+            base=0,
+            channel_multiplier=NT,
+        )
+        mask_a = const.tile([P, NT, NB], BF16)
+        nc.gpsimd.tensor_scalar(out=mask_a[:], in0=mask_a32[:], scalar1=1.0, scalar2=0.0, op0=ALU.mult, op1=ALU.add)
+        mask_r32 = const.tile([P, NT, NB, PACK], F32)
+        nc.gpsimd.memset(mask_r32[:], 0.0)
+        nc.gpsimd.affine_select(
+            out=mask_r32[:],
+            in_=mask_r32[:],
+            pattern=[[0, NT], [NB, NB], [0, PACK]],
+            compare_op=ALU.is_ge,
+            fill=NEG,
+            base=NB - 1,
+            channel_multiplier=-8,
+        )
+        nc.gpsimd.memset(mask_r32[:, 0, :, 0], 0.0)
+        mask_r = const.tile([P, S], BF16)
+        nc.gpsimd.tensor_scalar(
+            out=mask_r[:], in0=mask_r32[:].rearrange("r j a b -> r (j a b)"), scalar1=1.0, scalar2=0.0, op0=ALU.mult, op1=ALU.add
+        )
+
+        mask_own = const.tile([P, P], BF16)
+        nc.gpsimd.tensor_scalar(out=mask_own[:], in0=ident[:], scalar1=-1.0, scalar2=-NEG, op0=ALU.add, op1=ALU.mult)
+
+        head_of = const.tile([P, H], F32)
+        nc.vector.tensor_reduce(
+            out=head_of[:],
+            in_=ident[:, 0 : H * 8].rearrange("p (h x) -> p h x", x=8),
+            axis=AXIS_X,
+            op=ALU.add,
+        )
+        own_head = const.tile([P, HG], F32)
+        nc.vector.tensor_reduce(
+            out=own_head[:],
+            in_=ident[:].rearrange("p (a h) -> p h a", h=HG),
+            axis=AXIS_X,
+            op=ALU.add,
+        )
+
+        q_t = keep.tile([P, H, NT, P], BF16)
+        k_t = keep.tile([P, H, NT, P], BF16)
+        own_s = keep.tile([P, H, NT], F32)
+        top = keep.tile([P, H, NT], F32)
+        e_own = keep.tile([P, H, NT], F32)
+        rsum = keep.tile([P, H, NT], F32)
+        rinv = keep.tile([P, H, NT], F32)
+        e_pad = keep.tile([P, NT, PACK * P], BF16)
+        nc.vector.memset(e_pad[:, :, H * NB : PACK * P].bitcast(I32), 0)
+        ea_g = keep.tile([P, NT, P, PACK], BF16, align_bytes=64)
+        ea_c = keep.tile([P, NT, P], U32, align_bytes=64)
+        ea_s = keep.tile([P, NT, P], U8, align_bytes=64)
+        eb_g = [keep.tile([P, H, P, PACK], BF16, name="eb_g%d" % t, align_bytes=64) for t in range(PACK)]
+        v_c = keep.tile([P, 2, H, DK], U32, align_bytes=64)
+        v_s = keep.tile([P, 2, H, DK], U8, align_bytes=64)
+        va_raw = keep.tile([P, PACK, DK], BF16)
+        va_g = keep.tile([P, H, DK, PACK], BF16, align_bytes=64)
+        va_c = keep.tile([P, H, DK], U32, align_bytes=64)
+        va_s = keep.tile([P, H, DK], U8, align_bytes=64)
+        w_c = keep.tile([P, 2, D], U32, align_bytes=64)
+        w_s = keep.tile([P, 2, D], U8, align_bytes=64)
+        bias = keep.tile([P, D], BF16)
+        qs_pad = keep.tile([P, H, P], BF16)
+        nc.vector.memset(qs_pad[:].bitcast(I32), 0)
+        for t in range(PACK):
+            nc.vector.memset(eb_g[t][:].bitcast(I32), 0)
+        e_r = keep.tile([P, 2, NT, P], BF16)
+        top_r = keep.tile([P, 2, 2], F32)
+        shift_r = keep.tile([P, 2], F32)
+        rsum_r = keep.tile([P, 2, 2], F32)
+        rinv_r = keep.tile([P, 2], F32)
+        er_g = keep.tile([P, 2, 2, P, PACK], BF16, align_bytes=64)
+        er_c = keep.tile([P, 2, 2, P], U32, align_bytes=64)
+        er_s = keep.tile([P, 2, 2, P], U8, align_bytes=64)
+        ctx_r_t = keep.tile([P, 2, P], BF16)
+
+        def softmax_a(h0):
+            pair = slice(h0, h0 + 2)
+            a_ps = psum_f.tile([P, 2, NT, NB], F32, tag="acc")
+            s_a = stage.tile([P, 2, NT, NB], F32, tag="s_a")
+            for hh in range(2):
+                for j in range(NT):
+                    nc.tensor.matmul(out=a_ps[:, hh, j, :], lhsT=ident[:], rhs=mask_a[:, j, :], start=True, stop=False)
+                    nc.tensor.matmul(
+                        out=a_ps[:, hh, j, :],
+                        lhsT=q_t[:, h0 + hh, j, :],
+                        rhs=k_t[:, h0 + hh, 0, 0:P:PACK],
+                        start=False,
+                        stop=True,
+                    )
+            nc.vector.tensor_reduce(out=top[:, pair], in_=a_ps[:], axis=AXIS_X, op=ALU.max)
+            nc.vector.tensor_tensor(out=top[:, pair], in0=top[:, pair], in1=own_s[:, pair], op=ALU.max)
+            nc.vector.tensor_tensor(
+                out=s_a[:],
+                in0=a_ps[:],
+                in1=top[:, pair].unsqueeze(3).to_broadcast([P, 2, NT, NB]),
+                op=ALU.subtract,
+            )
+            nc.vector.tensor_tensor(out=own_s[:, pair], in0=own_s[:, pair], in1=top[:, pair], op=ALU.subtract)
+            nc.scalar.activation(out=s_a[:], in_=s_a[:], func=ACT.Exp, scale=SCALE)
+            nc.scalar.activation(out=e_own[:, pair], in_=own_s[:, pair], func=ACT.Exp, scale=SCALE)
+            nc.vector.tensor_reduce(out=rsum[:, pair], in_=s_a[:], axis=AXIS_X, op=ALU.add)
+            nc.vector.tensor_tensor(out=rsum[:, pair], in0=rsum[:, pair], in1=e_own[:, pair], op=ALU.add)
+            nc.vector.reciprocal(out=rinv[:, pair], in_=rsum[:, pair])
+            nc.scalar.copy(
+                out=e_pad[:, :, 0 : H * NB].rearrange("p j (h b) -> p h j b", h=H)[:, pair], in_=s_a[:]
+            )
+
+        def softmax_r(hg):
+            banks = []
+            for hl in range(HG):
+                h = hg * HG + hl
+                nc.vector.tensor_copy(out=qs_pad[:, h, hl:P:HG], in_=q_t[:, h, 0, 0:P:PACK])
+            for half in range(2):
+                r_ps = psum_f.tile([P, N_HALF], F32, tag="acc")
+                banks.append(r_ps)
+                cols = slice(half * N_HALF, (half + 1) * N_HALF)
+                nc.tensor.matmul(out=r_ps[:], lhsT=ident[:], rhs=mask_r[:, cols], start=True, stop=False)
+                for hl in range(HG):
+                    h = hg * HG + hl
+                    nc.tensor.matmul(
+                        out=r_ps[:],
+                        lhsT=qs_pad[:, h, :],
+                        rhs=k_t[:, h, half * PACK : (half + 1) * PACK, :].rearrange("d j p -> d (j p)"),
+                        start=False,
+                        stop=(hl == HG - 1),
+                    )
+                nc.vector.tensor_reduce(out=top_r[:, hg, half : half + 1], in_=r_ps[:], axis=AXIS_X, op=ALU.max)
+            nc.vector.tensor_tensor(
+                out=shift_r[:, hg : hg + 1], in0=top_r[:, hg, 0:1], in1=top_r[:, hg, 1:2], op=ALU.max
+            )
+            nc.vector.tensor_scalar(
+                out=shift_r[:, hg : hg + 1], in0=shift_r[:, hg : hg + 1], scalar1=-SCALE, scalar2=None, op0=ALU.mult
+            )
+            for half in range(2):
+                nc.scalar.activation(
+                    out=e_r[:, hg, half * PACK : (half + 1) * PACK, :].rearrange("r j p -> r (j p)"),
+                    in_=banks[half][:],
+                    func=ACT.Exp,
+                    bias=shift_r[:, hg : hg + 1],
+                    scale=SCALE,
+                    accum_out=rsum_r[:, hg, half : half + 1],
+                )
+            nc.vector.tensor_tensor(
+                out=rinv_r[:, hg : hg + 1], in0=rsum_r[:, hg, 0:1], in1=rsum_r[:, hg, 1:2], op=ALU.add
+            )
+            nc.vector.reciprocal(out=rinv_r[:, hg : hg + 1], in_=rinv_r[:, hg : hg + 1])
+
+        for h in range(H):
+            k_nat = loads.tile([P, NT, DK], BF16, tag="k_nat")
+            nc.sync.dma_start(out=k_nat[:], in_=kh[0, h].rearrange("(p j) d -> p j d", j=NT))
+            q_nat = loads.tile([P, NT, DK], BF16, tag="q_nat")
+            nc.sync.dma_start(out=q_nat[:], in_=qh[0, h].rearrange("(p j) d -> p j d", j=NT))
+            for nat, flipped in ((k_nat, k_t), (q_nat, q_t)):
+                for j0 in range(0, NT, PACK):
+                    bank = psum_t.tile([P, PACK, P], BF16, tag="tp")
+                    for j in range(j0, j0 + PACK):
+                        nc.tensor.transpose(bank[:, j - j0, :], nat[:, j, :], ident[:])
+                    nc.scalar.copy(out=flipped[:, h, j0 : j0 + PACK], in_=bank[:])
+            for j0 in range(0, NT, PACK):
+                d_ps = psum_o.tile([P, PACK, P], F32, tag="o_ps")
+                for j in range(j0, j0 + PACK):
+                    nc.tensor.matmul(out=d_ps[:, j - j0, :], lhsT=ident[:], rhs=mask_own[:], start=True, stop=False)
+                    nc.tensor.matmul(out=d_ps[:, j - j0, :], lhsT=q_t[:, h, j, :], rhs=k_t[:, h, j, :], start=False, stop=True)
+                nc.vector.tensor_reduce(out=own_s[:, h, j0 : j0 + PACK], in_=d_ps[:], axis=AXIS_X, op=ALU.max)
+            if h % 2 == 1:
+                softmax_a(h - 1)
+            if h % HG == HG - 1:
+                softmax_r(h // HG)
+
+        for j in range(NT):
+            bank = psum_t.tile([P, PACK, P], BF16, tag="tp")
+            for t in range(PACK):
+                nc.tensor.transpose(bank[:, t, :], e_pad[:, j, t : PACK * P : PACK], ident[:])
+            nc.scalar.copy(out=ea_g[:, j], in_=bank[:].rearrange("p t q -> p q t"))
+            quantise(nc, ea_c[:, j, :], ea_s[:, j, :], ea_g[:, j].rearrange("p q t -> p (q t)"))
+
+        nc.gpsimd.memset(va_raw[64:P], 0.0)
+        nc.sync.dma_start(
+            out=va_raw[0:64],
+            in_=vh[0].rearrange("h (x t s) d -> (h x) t s d", x=8, t=PACK)[:, :, 0, :],
+        )
+        va_w = keep.tile([P, DK, PACK], BF16)
+        nc.vector.tensor_copy(out=va_w[:], in_=va_raw[:].rearrange("p t d -> p d t"))
+        for h in range(H):
+            nc.vector.tensor_scalar(
+                out=va_g[:, h], in0=va_w[:], scalar1=head_of[:, h : h + 1], scalar2=None, op0=ALU.mult
+            )
+        quantise(
+            nc,
+            va_c[:].rearrange("p h d -> p (h d)"),
+            va_s[:].rearrange("p h d -> p (h d)"),
+            va_g[:].rearrange("p h d t -> p (h d t)"),
+        )
+        for h in range(H):
+            v_raw = loads.tile([P, 2, PACK, DK], BF16, tag="v_raw")
+            nc.sync.dma_start(
+                out=v_raw[:], in_=vh[0, h].rearrange("(p g t) d -> p g t d", g=2, t=PACK)
+            )
+            v_g = stage.tile([P, 2, DK, PACK], BF16, tag="v_g", align_bytes=64)
+            for g in range(2):
+                nc.scalar.copy(
+                    out=v_g[:, g].rearrange("p (c i) t -> p c t i", i=4),
+                    in_=v_raw[:, g].rearrange("p t (c i) -> p c t i", i=4),
+                )
+            for g in range(2):
+                quantise(nc, v_c[:, g, h, :], v_s[:, g, h, :], v_g[:, g].rearrange("p d t -> p (d t)"))
+
+        nc.sync.dma_start(out=bias[:], in_=bo.partition_broadcast(P))
+        for g in range(2):
+            for nh in range(2):
+                cols = slice(nh * N_HALF, (nh + 1) * N_HALF)
+                w_raw = loads.tile([P, PACK, N_HALF], BF16, tag="w_raw")
+                nc.sync.dma_start(
+                    out=w_raw[:],
+                    in_=Wo.rearrange("(g t p) n -> g p t n", g=2, t=PACK)[g][:, :, cols],
+                )
+                w_g = stage.tile([P, N_HALF, PACK], BF16, tag="w_g", align_bytes=64)
+                nc.vector.tensor_copy(
+                    out=w_g[:].rearrange("p (c i) t -> p c t i", i=4),
+                    in_=w_raw[:].rearrange("p t (c i) -> p c t i", i=4),
+                )
+                quantise(nc, w_c[:, g, cols], w_s[:, g, cols], w_g[:].rearrange("p n t -> p (n t)"))
+
+        out_rows = out[0].rearrange("(p j) n -> p j n", j=NT)
+        def query_tile(j):
+            t = j % PACK
+            for h in range(H):
+                if h < FILL_ON_SCALAR:
+                    nc.scalar.activation(
+                        out=eb_g[t][:, h, :, t], in_=ident[:], func=ACT.Copy, scale=e_own[:, h, j : j + 1]
+                    )
+                else:
+                    nc.vector.tensor_scalar(
+                        out=eb_g[t][:, h, :, t],
+                        in0=ident[:],
+                        scalar1=e_own[:, h, j : j + 1],
+                        scalar2=None,
+                        op0=ALU.mult,
+                    )
+            eb_c = stage.tile([P, H, P], U32, tag="eb_c", align_bytes=64)
+            eb_s = stage.tile([P, H, P], U8, tag="eb_s", align_bytes=64)
+            quantise(
+                nc,
+                eb_c[:].rearrange("p h c -> p (h c)"),
+                eb_s[:].rearrange("p h c -> p (h c)"),
+                eb_g[t][:].rearrange("p h c t -> p (h c t)"),
+            )
+            ctx_bf = stage.tile([P, H, DK], BF16, tag="ctx_bf")
+            for hg in range(2):
+                c_ps = psum_f.tile([P, HG, DK], F32, tag="acc")
+                for hl in range(HG):
+                    h = hg * HG + hl
+                    mx_pass(nc, c_ps[:, hl, :], ea_c[:, j, :], ea_s[:, j, :], va_c[:, h, :], va_s[:, h, :], True, False)
+                    mx_pass(
+                        nc, c_ps[:, hl, :], eb_c[:, h, :], eb_s[:, h, :],
+                        v_c[:, j // PACK, h, :], v_s[:, j // PACK, h, :], False, True,
+                    )
+                heads = slice(hg * HG, (hg + 1) * HG)
+                nc.vector.tensor_tensor(
+                    out=ctx_bf[:, heads],
+                    in0=c_ps[:],
+                    in1=rinv[:, heads, j].unsqueeze(2).to_broadcast([P, HG, DK]),
+                    op=ALU.mult,
+                )
+            c_g = stage.tile([P, 2, P, PACK], BF16, tag="c_g", align_bytes=64)
+            for hg in range(2):
+                bank = psum_t.tile([P, HG, P], BF16, tag="tp")
+                for hl in range(HG):
+                    nc.tensor.transpose(bank[:, hl, :], ctx_bf[:, hg * HG + hl, :], ident[:])
+                nc.scalar.copy(out=c_g[:, hg], in_=bank[:].rearrange("d t q -> d q t"))
+            if j == 0:
+                for hg in range(2):
+                    nc.vector.tensor_copy(
+                        out=c_g[:, hg, 0:P:PACK, :],
+                        in_=ctx_r_t[:, hg, :].rearrange("d (a t) -> d a t", t=HG),
+                    )
+            c_c = stage.tile([P, 2, P], U32, tag="c_c", align_bytes=64)
+            c_s = stage.tile([P, 2, P], U8, tag="c_s", align_bytes=64)
+            quantise(
+                nc,
+                c_c[:].rearrange("p g q -> p (g q)"),
+                c_s[:].rearrange("p g q -> p (g q)"),
+                c_g[:].rearrange("p g q t -> p (g q t)"),
+            )
+            o_sb = stage.tile([P, D], F32, tag="o_sb", bufs=3)
+            for nh in range(2):
+                cols = slice(nh * N_HALF, (nh + 1) * N_HALF)
+                o_ps = psum_o.tile([P, N_HALF], F32, tag="o_ps")
+                for g in range(2):
+                    mx_pass(nc, o_ps[:], c_c[:, g, :], c_s[:, g, :], w_c[:, g, cols], w_s[:, g, cols], g == 0, g == 1)
+                nc.vector.tensor_tensor(out=o_sb[:, cols], in0=o_ps[:], in1=bias[:, cols], op=ALU.add)
+            nc.sync.dma_start(out=out_rows[:, j, :], in_=o_sb[:])
+
+        for j in range(1, NT):
+            query_tile(j)
+        for hg in range(2):
+            for g in range(2):
+                bank = psum_t.tile([P, PACK, P], BF16, tag="tp")
+                for t in range(PACK):
+                    nc.tensor.transpose(bank[:, t, :], e_r[:, hg, g * PACK + t, :], ident[:])
+                nc.scalar.copy(out=er_g[:, hg, g], in_=bank[:].rearrange("p t r -> p r t"))
+            quantise(
+                nc,
+                er_c[:, hg].rearrange("p g r -> p (g r)"),
+                er_s[:, hg].rearrange("p g r -> p (g r)"),
+                er_g[:, hg].rearrange("p g r t -> p (g r t)"),
+            )
+            rc_ps = psum_f.tile([P, HG, DK], F32, tag="acc")
+            heads = slice(hg * HG, (hg + 1) * HG)
+            for g in range(2):
+                mx_pass(
+                    nc,
+                    rc_ps[:].rearrange("r h d -> r (h d)"),
+                    er_c[:, hg, g, :],
+                    er_s[:, hg, g, :],
+                    v_c[:, g, heads, :].rearrange("p h d -> p (h d)"),
+                    v_s[:, g, heads, :].rearrange("p h d -> p (h d)"),
+                    start=(g == 0),
+                    stop=(g == 1),
+                )
+            pick = stage.tile([P, HG], F32, tag="pick")
+            nc.vector.tensor_scalar(
+                out=pick[:], in0=own_head[:], scalar1=rinv_r[:, hg : hg + 1], scalar2=None, op0=ALU.mult
+            )
+            picked = stage.tile([P, HG, DK], F32, tag="picked")
+            nc.vector.tensor_tensor(
+                out=picked[:], in0=rc_ps[:], in1=pick[:].unsqueeze(2).to_broadcast([P, HG, DK]), op=ALU.mult
+            )
+            ctx_r32 = stage.tile([P, DK], F32, tag="ctx_r32")
+            nc.vector.tensor_reduce(
+                out=ctx_r32[:], in_=picked[:].rearrange("r h d -> r d h"), axis=AXIS_X, op=ALU.add
+            )
+            ctx_r = stage.tile([P, DK], BF16, tag="ctx_r")
+            nc.vector.tensor_copy(out=ctx_r[:], in_=ctx_r32[:])
+            bank = psum_t.tile([P, P], BF16, tag="tp")
+            nc.tensor.transpose(bank[:], ctx_r[:], ident[:])
+            nc.scalar.copy(out=ctx_r_t[:, hg, :], in_=bank[:])
+
+        query_tile(0)

@@ -25,7 +25,10 @@ PACK = 4
 HG = 4
 N_HALF = 512
 SCALE = 1.0 / math.sqrt(DK)
-FILL_ON_SCALAR = 6
+NQ = 4
+K_STEP = 160
+N_EARLY = 4
+N_KPAD = 3
 NEG = -1.0e30
 
 FLOPS = 3 * 2 * S * S * D
@@ -60,6 +63,12 @@ def tile_sparseattention_pa_kernel(tc, qh, kh, vh, Wo, bo, out):
 
         ident = const.tile([P, P], BF16)
         make_identity(nc, ident[:])
+        ident32 = const.tile([P, P], F32)
+        nc.vector.tensor_copy(out=ident32[:], in_=ident[:])
+
+        k_pads = [keep.tile([P, NT, NQ * K_STEP], BF16, name="k_pad%d" % i) for i in range(N_KPAD)]
+        for k_pad in k_pads:
+            nc.vector.memset(k_pad[:].bitcast(I32), 0)
 
         mask_a32 = const.tile([P, NT, NB], F32)
         nc.gpsimd.memset(mask_a32[:], 0.0)
@@ -72,9 +81,21 @@ def tile_sparseattention_pa_kernel(tc, qh, kh, vh, Wo, bo, out):
             base=0,
             channel_multiplier=NT,
         )
-        mask_a = const.tile([P, NT, NB], BF16)
-        nc.gpsimd.tensor_scalar(out=mask_a[:], in0=mask_a32[:], scalar1=1.0, scalar2=0.0, op0=ALU.mult, op1=ALU.add)
-        mask_r32 = const.tile([P, NT, NB, PACK], F32)
+        mask_s = const.tile([P, NT, 2, NB], BF16)
+        nc.vector.tensor_copy(out=mask_s[:, :, 0, :], in_=mask_a32[:])
+        own32 = const.tile([P, NB], F32)
+        nc.vector.tensor_reduce(
+            out=own32[:], in_=ident[:].rearrange("p (q c) -> p c q", q=NQ), axis=AXIS_X, op=ALU.add
+        )
+        nc.vector.tensor_scalar(
+            out=mask_s[:, :, 1, :],
+            in0=own32[:].unsqueeze(1).to_broadcast([P, NT, NB]),
+            scalar1=-1.0,
+            scalar2=-NEG,
+            op0=ALU.add,
+            op1=ALU.mult,
+        )
+        mask_r32 = stage.tile([P, NT, NB, PACK], F32, tag="w_g", align_bytes=64)
         nc.gpsimd.memset(mask_r32[:], 0.0)
         nc.gpsimd.affine_select(
             out=mask_r32[:],
@@ -91,8 +112,10 @@ def tile_sparseattention_pa_kernel(tc, qh, kh, vh, Wo, bo, out):
             out=mask_r[:], in0=mask_r32[:].rearrange("r j a b -> r (j a b)"), scalar1=1.0, scalar2=0.0, op0=ALU.mult, op1=ALU.add
         )
 
-        mask_own = const.tile([P, P], BF16)
-        nc.gpsimd.tensor_scalar(out=mask_own[:], in0=ident[:], scalar1=-1.0, scalar2=-NEG, op0=ALU.add, op1=ALU.mult)
+        diag = const.tile([P, PACK, P, PACK], BF16)
+        nc.vector.memset(diag[:].bitcast(I32), 0)
+        for t in range(PACK):
+            nc.vector.tensor_copy(out=diag[:, t, :, t], in_=ident[:])
 
         head_of = const.tile([P, H], F32)
         nc.vector.tensor_reduce(
@@ -109,23 +132,25 @@ def tile_sparseattention_pa_kernel(tc, qh, kh, vh, Wo, bo, out):
             op=ALU.add,
         )
 
-        q_t = keep.tile([P, H, NT, P], BF16)
-        k_t = keep.tile([P, H, NT, P], BF16)
-        own_s = keep.tile([P, H, NT], F32)
+        highs = keep.tile([P, H, NT, 2], F32)
         top = keep.tile([P, H, NT], F32)
+        shift = keep.tile([P, H, NT], F32)
+        own_s = keep.tile([P, H, NT], F32)
         e_own = keep.tile([P, H, NT], F32)
+        rsum_a = keep.tile([P, H, NT], F32)
         rsum = keep.tile([P, H, NT], F32)
         rinv = keep.tile([P, H, NT], F32)
         e_pad = keep.tile([P, NT, PACK * P], BF16)
         nc.vector.memset(e_pad[:, :, H * NB : PACK * P].bitcast(I32), 0)
-        ea_g = keep.tile([P, NT, P, PACK], BF16, align_bytes=64)
         ea_c = keep.tile([P, NT, P], U32, align_bytes=64)
         ea_s = keep.tile([P, NT, P], U8, align_bytes=64)
-        eb_g = [keep.tile([P, H, P, PACK], BF16, name="eb_g%d" % t, align_bytes=64) for t in range(PACK)]
+        eb_c = keep.tile([P, N_EARLY, NT, P], U32, align_bytes=64)
+        eb_s = keep.tile([P, N_EARLY, NT, P], U8, align_bytes=64)
+        ebl_c = keep.tile([P, NT, H - N_EARLY, P], U32, align_bytes=64)
+        ebl_s = keep.tile([P, NT, H - N_EARLY, P], U8, align_bytes=64)
         v_c = keep.tile([P, 2, H, DK], U32, align_bytes=64)
         v_s = keep.tile([P, 2, H, DK], U8, align_bytes=64)
         va_raw = keep.tile([P, PACK, DK], BF16)
-        va_g = keep.tile([P, H, DK, PACK], BF16, align_bytes=64)
         va_c = keep.tile([P, H, DK], U32, align_bytes=64)
         va_s = keep.tile([P, H, DK], U8, align_bytes=64)
         w_c = keep.tile([P, 2, D], U32, align_bytes=64)
@@ -133,8 +158,6 @@ def tile_sparseattention_pa_kernel(tc, qh, kh, vh, Wo, bo, out):
         bias = keep.tile([P, D], BF16)
         qs_pad = keep.tile([P, H, P], BF16)
         nc.vector.memset(qs_pad[:].bitcast(I32), 0)
-        for t in range(PACK):
-            nc.vector.memset(eb_g[t][:].bitcast(I32), 0)
         e_r = keep.tile([P, 2, NT, P], BF16)
         top_r = keep.tile([P, 2, 2], F32)
         shift_r = keep.tile([P, 2], F32)
@@ -143,60 +166,95 @@ def tile_sparseattention_pa_kernel(tc, qh, kh, vh, Wo, bo, out):
         er_g = keep.tile([P, 2, 2, P, PACK], BF16, align_bytes=64)
         er_c = keep.tile([P, 2, 2, P], U32, align_bytes=64)
         er_s = keep.tile([P, 2, 2, P], U8, align_bytes=64)
-        ctx_r_t = keep.tile([P, 2, P], BF16)
 
-        def softmax_a(h0):
-            pair = slice(h0, h0 + 2)
-            a_ps = psum_f.tile([P, 2, NT, NB], F32, tag="acc")
-            s_a = stage.tile([P, 2, NT, NB], F32, tag="s_a")
-            for hh in range(2):
-                for j in range(NT):
-                    nc.tensor.matmul(out=a_ps[:, hh, j, :], lhsT=ident[:], rhs=mask_a[:, j, :], start=True, stop=False)
+        q_ts = {}
+        r_banks = {}
+
+        def transposed(h):
+            k_nat = loads.tile([P, NT, DK], BF16, tag="k_nat")
+            nc.sync.dma_start(out=k_nat[:], in_=kh[0, h].rearrange("(p j) d -> p j d", j=NT))
+            q_nat = loads.tile([P, NT, DK], BF16, tag="q_nat")
+            nc.sync.dma_start(out=q_nat[:], in_=qh[0, h].rearrange("(p j) d -> p j d", j=NT))
+            q_t = loads.tile([P, NT, P], BF16, tag="q_t")
+            q_ts[h] = q_t
+            k_pad = k_pads[h % N_KPAD]
+            for j0 in range(0, NT, PACK):
+                bank = psum_t.tile([P, PACK, P], BF16, tag="tp")
+                for j in range(j0, j0 + PACK):
+                    nc.tensor.transpose(bank[:, j - j0, :], k_nat[:, j, :], ident[:])
+                nc.scalar.copy(
+                    out=k_pad[:, j0 : j0 + PACK].rearrange("d j (q c) -> d j q c", q=NQ)[:, :, :, 0:NB],
+                    in_=bank[:].rearrange("d j (q c) -> d j q c", q=NQ),
+                )
+            for j0 in range(0, NT, PACK):
+                bank = psum_t.tile([P, PACK, P], BF16, tag="tp")
+                for j in range(j0, j0 + PACK):
+                    nc.tensor.transpose(bank[:, j - j0, :], q_nat[:, j, :], ident[:])
+                nc.scalar.copy(out=q_t[:, j0 : j0 + PACK], in_=bank[:])
+
+        def softmax(h):
+            q_t, k_pad = q_ts[h], k_pads[h % N_KPAD]
+            s_ps = psum_f.tile([P, NT, 2, NB], F32, tag="acc")
+            nc.tensor.matmul(
+                out=s_ps[:].rearrange("p j i c -> p (j i c)"),
+                lhsT=ident[:],
+                rhs=mask_s[:].rearrange("p j i c -> p (j i c)"),
+                start=True,
+                stop=False,
+            )
+            for j in range(NT):
+                nc.tensor.matmul(
+                    out=s_ps[:, j, 0, :],
+                    lhsT=q_t[:, j, :],
+                    rhs=k_pad[:, 0, :].rearrange("d (q c) -> d q c", q=NQ)[:, :, 0:NB:PACK],
+                    start=False,
+                    stop=False,
+                )
+                for q in range(NQ):
                     nc.tensor.matmul(
-                        out=a_ps[:, hh, j, :],
-                        lhsT=q_t[:, h0 + hh, j, :],
-                        rhs=k_t[:, h0 + hh, 0, 0:P:PACK],
+                        out=s_ps[:, j, 1, :],
+                        lhsT=k_pad[:, j, q * P : (q + 1) * P],
+                        rhs=q_t[:, j, q * NB : (q + 1) * NB],
                         start=False,
-                        stop=True,
+                        stop=(j == NT - 1 and q == NQ - 1),
                     )
-            nc.vector.tensor_reduce(out=top[:, pair], in_=a_ps[:], axis=AXIS_X, op=ALU.max)
-            nc.vector.tensor_tensor(out=top[:, pair], in0=top[:, pair], in1=own_s[:, pair], op=ALU.max)
-            nc.vector.tensor_tensor(
-                out=s_a[:],
-                in0=a_ps[:],
-                in1=top[:, pair].unsqueeze(3).to_broadcast([P, 2, NT, NB]),
-                op=ALU.subtract,
-            )
-            nc.vector.tensor_tensor(out=own_s[:, pair], in0=own_s[:, pair], in1=top[:, pair], op=ALU.subtract)
-            nc.scalar.activation(out=s_a[:], in_=s_a[:], func=ACT.Exp, scale=SCALE)
-            nc.scalar.activation(out=e_own[:, pair], in_=own_s[:, pair], func=ACT.Exp, scale=SCALE)
-            nc.vector.tensor_reduce(out=rsum[:, pair], in_=s_a[:], axis=AXIS_X, op=ALU.add)
-            nc.vector.tensor_tensor(out=rsum[:, pair], in0=rsum[:, pair], in1=e_own[:, pair], op=ALU.add)
-            nc.vector.reciprocal(out=rinv[:, pair], in_=rsum[:, pair])
-            nc.scalar.copy(
-                out=e_pad[:, :, 0 : H * NB].rearrange("p j (h b) -> p h j b", h=H)[:, pair], in_=s_a[:]
-            )
+            nc.vector.tensor_reduce(out=highs[:, h], in_=s_ps[:], axis=AXIS_X, op=ALU.max)
+            nc.vector.tensor_tensor(out=top[:, h], in0=highs[:, h, :, 0], in1=highs[:, h, :, 1], op=ALU.max)
+            nc.vector.tensor_scalar(out=shift[:, h], in0=top[:, h], scalar1=-SCALE, scalar2=None, op0=ALU.mult)
+            nc.vector.tensor_tensor(out=own_s[:, h], in0=highs[:, h, :, 1], in1=top[:, h], op=ALU.subtract)
+            nc.scalar.activation(out=e_own[:, h], in_=own_s[:, h], func=ACT.Exp, scale=SCALE)
+            for j in range(NT):
+                nc.scalar.activation(
+                    out=e_pad[:, j, h * NB : (h + 1) * NB],
+                    in_=s_ps[:, j, 0, :],
+                    func=ACT.Exp,
+                    bias=shift[:, h, j : j + 1],
+                    scale=SCALE,
+                    accum_out=rsum_a[:, h, j : j + 1],
+                )
 
-        def softmax_r(hg):
-            banks = []
-            for hl in range(HG):
-                h = hg * HG + hl
-                nc.vector.tensor_copy(out=qs_pad[:, h, hl:P:HG], in_=q_t[:, h, 0, 0:P:PACK])
+        def part_r_scores(h):
+            hg, hl = divmod(h, HG)
+            q_t, k_pad = q_ts[h], k_pads[h % N_KPAD]
+            nc.vector.tensor_copy(out=qs_pad[:, h, hl:P:HG], in_=q_t[:, 0, 0:P:PACK])
             for half in range(2):
-                r_ps = psum_f.tile([P, N_HALF], F32, tag="acc")
-                banks.append(r_ps)
-                cols = slice(half * N_HALF, (half + 1) * N_HALF)
-                nc.tensor.matmul(out=r_ps[:], lhsT=ident[:], rhs=mask_r[:, cols], start=True, stop=False)
-                for hl in range(HG):
-                    h = hg * HG + hl
-                    nc.tensor.matmul(
-                        out=r_ps[:],
-                        lhsT=qs_pad[:, h, :],
-                        rhs=k_t[:, h, half * PACK : (half + 1) * PACK, :].rearrange("d j p -> d (j p)"),
-                        start=False,
-                        stop=(hl == HG - 1),
-                    )
-                nc.vector.tensor_reduce(out=top_r[:, hg, half : half + 1], in_=r_ps[:], axis=AXIS_X, op=ALU.max)
+                if hl == 0:
+                    r_banks[hg, half] = psum_o.tile([P, N_HALF], F32, tag="o_ps", name="r_ps%d" % half)
+                    cols = slice(half * N_HALF, (half + 1) * N_HALF)
+                    nc.tensor.matmul(out=r_banks[hg, half][:], lhsT=ident[:], rhs=mask_r[:, cols], start=True, stop=False)
+                nc.tensor.matmul(
+                    out=r_banks[hg, half][:].rearrange("r (j q c) -> r j q c", j=PACK, q=NQ),
+                    lhsT=qs_pad[:, h, :],
+                    rhs=k_pad[:, half * PACK : (half + 1) * PACK].rearrange("d j (q c) -> d j q c", q=NQ)[:, :, :, 0:NB],
+                    start=False,
+                    stop=(hl == HG - 1),
+                )
+            if hl < HG - 1:
+                return
+            for half in range(2):
+                nc.vector.tensor_reduce(
+                    out=top_r[:, hg, half : half + 1], in_=r_banks[hg, half][:], axis=AXIS_X, op=ALU.max
+                )
             nc.vector.tensor_tensor(
                 out=shift_r[:, hg : hg + 1], in0=top_r[:, hg, 0:1], in1=top_r[:, hg, 1:2], op=ALU.max
             )
@@ -206,7 +264,7 @@ def tile_sparseattention_pa_kernel(tc, qh, kh, vh, Wo, bo, out):
             for half in range(2):
                 nc.scalar.activation(
                     out=e_r[:, hg, half * PACK : (half + 1) * PACK, :].rearrange("r j p -> r (j p)"),
-                    in_=banks[half][:],
+                    in_=r_banks[hg, half][:],
                     func=ACT.Exp,
                     bias=shift_r[:, hg : hg + 1],
                     scale=SCALE,
@@ -217,57 +275,43 @@ def tile_sparseattention_pa_kernel(tc, qh, kh, vh, Wo, bo, out):
             )
             nc.vector.reciprocal(out=rinv_r[:, hg : hg + 1], in_=rinv_r[:, hg : hg + 1])
 
-        for h in range(H):
-            k_nat = loads.tile([P, NT, DK], BF16, tag="k_nat")
-            nc.sync.dma_start(out=k_nat[:], in_=kh[0, h].rearrange("(p j) d -> p j d", j=NT))
-            q_nat = loads.tile([P, NT, DK], BF16, tag="q_nat")
-            nc.sync.dma_start(out=q_nat[:], in_=qh[0, h].rearrange("(p j) d -> p j d", j=NT))
-            for nat, flipped in ((k_nat, k_t), (q_nat, q_t)):
-                for j0 in range(0, NT, PACK):
-                    bank = psum_t.tile([P, PACK, P], BF16, tag="tp")
-                    for j in range(j0, j0 + PACK):
-                        nc.tensor.transpose(bank[:, j - j0, :], nat[:, j, :], ident[:])
-                    nc.scalar.copy(out=flipped[:, h, j0 : j0 + PACK], in_=bank[:])
-            for j0 in range(0, NT, PACK):
-                d_ps = psum_o.tile([P, PACK, P], F32, tag="o_ps")
-                for j in range(j0, j0 + PACK):
-                    nc.tensor.matmul(out=d_ps[:, j - j0, :], lhsT=ident[:], rhs=mask_own[:], start=True, stop=False)
-                    nc.tensor.matmul(out=d_ps[:, j - j0, :], lhsT=q_t[:, h, j, :], rhs=k_t[:, h, j, :], start=False, stop=True)
-                nc.vector.tensor_reduce(out=own_s[:, h, j0 : j0 + PACK], in_=d_ps[:], axis=AXIS_X, op=ALU.max)
-            if h % 2 == 1:
-                softmax_a(h - 1)
-            if h % HG == HG - 1:
-                softmax_r(h // HG)
-
-        for j in range(NT):
-            bank = psum_t.tile([P, PACK, P], BF16, tag="tp")
-            for t in range(PACK):
-                nc.tensor.transpose(bank[:, t, :], e_pad[:, j, t : PACK * P : PACK], ident[:])
-            nc.scalar.copy(out=ea_g[:, j], in_=bank[:].rearrange("p t q -> p q t"))
-            quantise(nc, ea_c[:, j, :], ea_s[:, j, :], ea_g[:, j].rearrange("p q t -> p (q t)"))
-
-        nc.gpsimd.memset(va_raw[64:P], 0.0)
-        nc.sync.dma_start(
-            out=va_raw[0:64],
-            in_=vh[0].rearrange("h (x t s) d -> (h x) t s d", x=8, t=PACK)[:, :, 0, :],
-        )
-        va_w = keep.tile([P, DK, PACK], BF16)
-        nc.vector.tensor_copy(out=va_w[:], in_=va_raw[:].rearrange("p t d -> p d t"))
-        for h in range(H):
-            nc.vector.tensor_scalar(
-                out=va_g[:, h], in0=va_w[:], scalar1=head_of[:, h : h + 1], scalar2=None, op0=ALU.mult
+        def part_b_operand(h):
+            eb_g = stage.tile([P, NT, P, PACK], BF16, tag="eb_g", align_bytes=64)
+            for j in range(NT):
+                nc.vector.tensor_scalar(
+                    out=eb_g[:, j].rearrange("p c t -> p (c t)"),
+                    in0=diag[:, j % PACK].rearrange("p c t -> p (c t)"),
+                    scalar1=e_own[:, h, j : j + 1],
+                    scalar2=None,
+                    op0=ALU.mult,
+                )
+            quantise(
+                nc,
+                eb_c[:, h].rearrange("p j c -> p (j c)"),
+                eb_s[:, h].rearrange("p j c -> p (j c)"),
+                eb_g[:].rearrange("p j c t -> p (j c t)"),
             )
-        quantise(
-            nc,
-            va_c[:].rearrange("p h d -> p (h d)"),
-            va_s[:].rearrange("p h d -> p (h d)"),
-            va_g[:].rearrange("p h d t -> p (h d t)"),
-        )
-        for h in range(H):
+
+        def part_b_tile(j):
+            eb_g = stage.tile([P, H - N_EARLY, P, PACK], BF16, tag="eb_g", align_bytes=64)
+            for h in range(N_EARLY, H):
+                nc.vector.tensor_scalar(
+                    out=eb_g[:, h - N_EARLY].rearrange("p c t -> p (c t)"),
+                    in0=diag[:, j % PACK].rearrange("p c t -> p (c t)"),
+                    scalar1=e_own[:, h, j : j + 1],
+                    scalar2=None,
+                    op0=ALU.mult,
+                )
+            quantise(
+                nc,
+                ebl_c[:, j].rearrange("p h c -> p (h c)"),
+                ebl_s[:, j].rearrange("p h c -> p (h c)"),
+                eb_g[:].rearrange("p h c t -> p (h c t)"),
+            )
+
+        def values(h):
             v_raw = loads.tile([P, 2, PACK, DK], BF16, tag="v_raw")
-            nc.sync.dma_start(
-                out=v_raw[:], in_=vh[0, h].rearrange("(p g t) d -> p g t d", g=2, t=PACK)
-            )
+            nc.sync.dma_start(out=v_raw[:], in_=vh[0, h].rearrange("(p g t) d -> p g t d", g=2, t=PACK))
             v_g = stage.tile([P, 2, DK, PACK], BF16, tag="v_g", align_bytes=64)
             for g in range(2):
                 nc.scalar.copy(
@@ -277,75 +321,118 @@ def tile_sparseattention_pa_kernel(tc, qh, kh, vh, Wo, bo, out):
             for g in range(2):
                 quantise(nc, v_c[:, g, h, :], v_s[:, g, h, :], v_g[:, g].rearrange("p d t -> p (d t)"))
 
-        nc.sync.dma_start(out=bias[:], in_=bo.partition_broadcast(P))
-        for g in range(2):
+        def strided_values():
+            nc.gpsimd.memset(va_raw[64:P], 0.0)
+            nc.sync.dma_start(
+                out=va_raw[0:64],
+                in_=vh[0].rearrange("h (x t s) d -> (h x) t s d", x=8, t=PACK)[:, :, 0, :],
+            )
+            va_w = keep.tile([P, DK, PACK], BF16)
+            va_g = stage.tile([P, H, DK, PACK], BF16, tag="eb_g", align_bytes=64)
+            nc.vector.tensor_copy(out=va_w[:], in_=va_raw[:].rearrange("p t d -> p d t"))
+            for h in range(H):
+                nc.vector.tensor_scalar(
+                    out=va_g[:, h], in0=va_w[:], scalar1=head_of[:, h : h + 1], scalar2=None, op0=ALU.mult
+                )
+            quantise(
+                nc,
+                va_c[:].rearrange("p h d -> p (h d)"),
+                va_s[:].rearrange("p h d -> p (h d)"),
+                va_g[:].rearrange("p h d t -> p (h d t)"),
+            )
+
+        def weights(g):
+            w_raw = loads.tile([P, PACK, D], BF16, tag="w_raw", bufs=2)
+            nc.sync.dma_start(
+                out=w_raw[:].rearrange("p (u e) n -> p u e n", u=2),
+                in_=Wo.rearrange("(g u p e) n -> g p u e n", g=2, u=2, e=2)[g],
+            )
             for nh in range(2):
                 cols = slice(nh * N_HALF, (nh + 1) * N_HALF)
-                w_raw = loads.tile([P, PACK, N_HALF], BF16, tag="w_raw")
-                nc.sync.dma_start(
-                    out=w_raw[:],
-                    in_=Wo.rearrange("(g t p) n -> g p t n", g=2, t=PACK)[g][:, :, cols],
-                )
                 w_g = stage.tile([P, N_HALF, PACK], BF16, tag="w_g", align_bytes=64)
                 nc.vector.tensor_copy(
                     out=w_g[:].rearrange("p (c i) t -> p c t i", i=4),
-                    in_=w_raw[:].rearrange("p t (c i) -> p c t i", i=4),
+                    in_=w_raw[:, :, cols].rearrange("p t (c i) -> p c t i", i=4),
                 )
                 quantise(nc, w_c[:, g, cols], w_s[:, g, cols], w_g[:].rearrange("p n t -> p (n t)"))
 
-        out_rows = out[0].rearrange("(p j) n -> p j n", j=NT)
-        def query_tile(j):
-            t = j % PACK
-            for h in range(H):
-                if h < FILL_ON_SCALAR:
-                    nc.scalar.activation(
-                        out=eb_g[t][:, h, :, t], in_=ident[:], func=ACT.Copy, scale=e_own[:, h, j : j + 1]
-                    )
-                else:
-                    nc.vector.tensor_scalar(
-                        out=eb_g[t][:, h, :, t],
-                        in0=ident[:],
-                        scalar1=e_own[:, h, j : j + 1],
-                        scalar2=None,
-                        op0=ALU.mult,
-                    )
-            eb_c = stage.tile([P, H, P], U32, tag="eb_c", align_bytes=64)
-            eb_s = stage.tile([P, H, P], U8, tag="eb_s", align_bytes=64)
+        for h in range(H + 2):
+            if h < H:
+                transposed(h)
+            if 1 <= h <= H:
+                softmax(h - 1)
+            if h >= 2:
+                part_r_scores(h - 2)
+                if h - 2 < N_EARLY:
+                    part_b_operand(h - 2)
+            if 1 <= h <= H:
+                values(h - 1)
+        strided_values()
+        nc.sync.dma_start(out=bias[:], in_=bo.partition_broadcast(P))
+        for g in range(2):
+            weights(g)
+        nc.vector.tensor_tensor(out=rsum[:], in0=rsum_a[:], in1=e_own[:], op=ALU.add)
+        nc.vector.reciprocal(out=rinv[:], in_=rsum[:])
+
+        for j0 in range(0, NT, 2):
+            ea_g = stage.tile([P, 2, P, PACK], BF16, tag="ea_g", align_bytes=64)
+            bank = psum_t.tile([P, 2, 2, P], F32, tag="tp")
+            for j in range(j0, j0 + 2):
+                words = e_pad[:, j, :].bitcast(F32)
+                for u in range(2):
+                    nc.tensor.transpose(bank[:, j - j0, u, :], words[:, u : 2 * P : 2], ident32[:])
+            nc.scalar.copy(
+                out=ea_g[:].rearrange("p j q t -> p j (q t)").bitcast(F32).rearrange("p j (q u) -> p j q u", u=2),
+                in_=bank[:].rearrange("p j u q -> p j q u"),
+            )
             quantise(
                 nc,
-                eb_c[:].rearrange("p h c -> p (h c)"),
-                eb_s[:].rearrange("p h c -> p (h c)"),
-                eb_g[t][:].rearrange("p h c t -> p (h c t)"),
+                ea_c[:, j0 : j0 + 2, :].rearrange("p j q -> p (j q)"),
+                ea_s[:, j0 : j0 + 2, :].rearrange("p j q -> p (j q)"),
+                ea_g[:].rearrange("p j q t -> p (j q t)"),
             )
+
+        out_rows = out[0].rearrange("(p j) n -> p j n", j=NT)
+        ctx_r_w = []
+
+        def query_tile(j):
             ctx_bf = stage.tile([P, H, DK], BF16, tag="ctx_bf")
             for hg in range(2):
+                heads = slice(hg * HG, (hg + 1) * HG)
                 c_ps = psum_f.tile([P, HG, DK], F32, tag="acc")
+                mx_pass(
+                    nc, c_ps[:].rearrange("p h d -> p (h d)"), ea_c[:, j, :], ea_s[:, j, :],
+                    va_c[:, heads, :].rearrange("p h d -> p (h d)"), va_s[:, heads, :].rearrange("p h d -> p (h d)"), True, False,
+                )
                 for hl in range(HG):
                     h = hg * HG + hl
-                    mx_pass(nc, c_ps[:, hl, :], ea_c[:, j, :], ea_s[:, j, :], va_c[:, h, :], va_s[:, h, :], True, False)
+                    if h < N_EARLY:
+                        e_codes, e_scales = eb_c[:, h, j, :], eb_s[:, h, j, :]
+                    else:
+                        e_codes, e_scales = ebl_c[:, j, h - N_EARLY, :], ebl_s[:, j, h - N_EARLY, :]
                     mx_pass(
-                        nc, c_ps[:, hl, :], eb_c[:, h, :], eb_s[:, h, :],
-                        v_c[:, j // PACK, h, :], v_s[:, j // PACK, h, :], False, True,
+                        nc, c_ps[:, hl, :], e_codes, e_scales,
+                        v_c[:, j // PACK, h, :], v_s[:, j // PACK, h, :], False, hl == HG - 1,
                     )
-                heads = slice(hg * HG, (hg + 1) * HG)
-                nc.vector.tensor_tensor(
-                    out=ctx_bf[:, heads],
-                    in0=c_ps[:],
-                    in1=rinv[:, heads, j].unsqueeze(2).to_broadcast([P, HG, DK]),
-                    op=ALU.mult,
-                )
-            c_g = stage.tile([P, 2, P, PACK], BF16, tag="c_g", align_bytes=64)
-            for hg in range(2):
-                bank = psum_t.tile([P, HG, P], BF16, tag="tp")
                 for hl in range(HG):
-                    nc.tensor.transpose(bank[:, hl, :], ctx_bf[:, hg * HG + hl, :], ident[:])
-                nc.scalar.copy(out=c_g[:, hg], in_=bank[:].rearrange("d t q -> d q t"))
+                    h = hg * HG + hl
+                    nc.scalar.activation(out=ctx_bf[:, h, :], in_=c_ps[:, hl, :], func=ACT.Copy, scale=rinv[:, h, j : j + 1])
+            bank = psum_t.tile([P, 2, 2, P], F32, tag="tp")
+            for hg in range(2):
+                words = ctx_bf[:, hg * HG : (hg + 1) * HG, :].rearrange("p h d -> p (h d)").bitcast(F32)
+                for u in range(2):
+                    nc.tensor.transpose(bank[:, hg, u, :], words[:, u * P : (u + 1) * P], ident32[:])
+            c_g = stage.tile([P, 2, P, PACK], BF16, tag="c_g", align_bytes=64)
+            c_gw = c_g[:].rearrange("p g q t -> p (g q t)").bitcast(F32).rearrange("p (g q u) -> p g q u", g=2, u=2)
+            nc.scalar.copy(out=c_gw, in_=bank[:].rearrange("p g u q -> p g q u"))
             if j == 0:
                 for hg in range(2):
-                    nc.vector.tensor_copy(
-                        out=c_g[:, hg, 0:P:PACK, :],
-                        in_=ctx_r_t[:, hg, :].rearrange("d (a t) -> d a t", t=HG),
-                    )
+                    for f in range(2):
+                        rows = slice(64 * f, 64 * (f + 1))
+                        nc.scalar.copy(
+                            out=c_gw[rows, hg, 0:P:PACK, :],
+                            in_=ctx_r_w[hg][rows].rearrange("d (a u f) -> d a u f", u=2, f=2)[:, :, :, f],
+                        )
             c_c = stage.tile([P, 2, P], U32, tag="c_c", align_bytes=64)
             c_s = stage.tile([P, 2, P], U8, tag="c_s", align_bytes=64)
             quantise(
@@ -363,9 +450,7 @@ def tile_sparseattention_pa_kernel(tc, qh, kh, vh, Wo, bo, out):
                 nc.vector.tensor_tensor(out=o_sb[:, cols], in0=o_ps[:], in1=bias[:, cols], op=ALU.add)
             nc.sync.dma_start(out=out_rows[:, j, :], in_=o_sb[:])
 
-        for j in range(1, NT):
-            query_tile(j)
-        for hg in range(2):
+        def part_r(hg):
             for g in range(2):
                 bank = psum_t.tile([P, PACK, P], BF16, tag="tp")
                 for t in range(PACK):
@@ -398,14 +483,19 @@ def tile_sparseattention_pa_kernel(tc, qh, kh, vh, Wo, bo, out):
             nc.vector.tensor_tensor(
                 out=picked[:], in0=rc_ps[:], in1=pick[:].unsqueeze(2).to_broadcast([P, HG, DK]), op=ALU.mult
             )
-            ctx_r32 = stage.tile([P, DK], F32, tag="ctx_r32")
-            nc.vector.tensor_reduce(
-                out=ctx_r32[:], in_=picked[:].rearrange("r h d -> r d h"), axis=AXIS_X, op=ALU.add
-            )
-            ctx_r = stage.tile([P, DK], BF16, tag="ctx_r")
-            nc.vector.tensor_copy(out=ctx_r[:], in_=ctx_r32[:])
-            bank = psum_t.tile([P, P], BF16, tag="tp")
-            nc.tensor.transpose(bank[:], ctx_r[:], ident[:])
-            nc.scalar.copy(out=ctx_r_t[:, hg, :], in_=bank[:])
+            ctx_r = stage.tile([P, 2, DK], BF16, tag="ctx_r")
+            nc.vector.tensor_tensor(out=ctx_r[:], in0=picked[:, 0:2, :], in1=picked[:, 2:4, :], op=ALU.add)
+            bank = psum_t.tile([P, P], F32, tag="tp")
+            nc.tensor.transpose(bank[:], ctx_r[:].rearrange("r f d -> r (f d)").bitcast(F32), ident32[:])
+            ctx_w = keep.tile([P, P], F32, name="ctx_r_w%d" % hg)
+            nc.scalar.copy(out=ctx_w[:], in_=bank[:])
+            ctx_r_w.append(ctx_w)
 
-        query_tile(0)
+        order = list(range(1, NT)) + [0]
+        part_b_tile(order[0])
+        for i, j in enumerate(order):
+            if i + 1 < NT:
+                part_b_tile(order[i + 1])
+            query_tile(j)
+            if i in (2, 3):
+                part_r(i - 2)

@@ -63,12 +63,6 @@ def tile_sparseattention_pa_kernel(tc, qh, kh, vh, Wo, bo, out):
 
         ident = const.tile([P, P], BF16)
         make_identity(nc, ident[:])
-        ident32 = const.tile([P, P], F32)
-        nc.vector.tensor_copy(out=ident32[:], in_=ident[:])
-
-        k_pads = [keep.tile([P, NT, NQ * K_STEP], BF16, name="k_pad%d" % i) for i in range(N_KPAD)]
-        for k_pad in k_pads:
-            nc.vector.memset(k_pad[:].bitcast(I32), 0)
 
         mask_a32 = const.tile([P, NT, NB], F32)
         nc.gpsimd.memset(mask_a32[:], 0.0)
@@ -95,6 +89,11 @@ def tile_sparseattention_pa_kernel(tc, qh, kh, vh, Wo, bo, out):
             op0=ALU.add,
             op1=ALU.mult,
         )
+        k_pads = [keep.tile([P, NT, NQ * K_STEP], BF16, name="k_pad%d" % i) for i in range(N_KPAD)]
+        for i, k_pad in enumerate(k_pads):
+            engine = nc.vector if i == 0 else nc.gpsimd
+            engine.memset(k_pad[:].bitcast(I32), 0)
+
         mask_r32 = stage.tile([P, NT, NB, PACK], F32, tag="w_g", align_bytes=64)
         nc.gpsimd.memset(mask_r32[:], 0.0)
         nc.gpsimd.affine_select(
@@ -112,8 +111,11 @@ def tile_sparseattention_pa_kernel(tc, qh, kh, vh, Wo, bo, out):
             out=mask_r[:], in0=mask_r32[:].rearrange("r j a b -> r (j a b)"), scalar1=1.0, scalar2=0.0, op0=ALU.mult, op1=ALU.add
         )
 
+        ident32 = const.tile([P, P], F32)
+        nc.vector.tensor_copy(out=ident32[:], in_=ident[:])
+
         diag = const.tile([P, PACK, P, PACK], BF16)
-        nc.vector.memset(diag[:].bitcast(I32), 0)
+        nc.gpsimd.memset(diag[:].bitcast(I32), 0)
         for t in range(PACK):
             nc.vector.tensor_copy(out=diag[:, t, :, t], in_=ident[:])
 
@@ -141,7 +143,7 @@ def tile_sparseattention_pa_kernel(tc, qh, kh, vh, Wo, bo, out):
         rsum = keep.tile([P, H, NT], F32)
         rinv = keep.tile([P, H, NT], F32)
         e_pad = keep.tile([P, NT, PACK * P], BF16)
-        nc.vector.memset(e_pad[:, :, H * NB : PACK * P].bitcast(I32), 0)
+        nc.gpsimd.memset(e_pad[:, :, H * NB : PACK * P].bitcast(I32), 0)
         ea_c = keep.tile([P, NT, P], U32, align_bytes=64)
         ea_s = keep.tile([P, NT, P], U8, align_bytes=64)
         eb_c = keep.tile([P, N_EARLY, NT, P], U32, align_bytes=64)
@@ -157,7 +159,7 @@ def tile_sparseattention_pa_kernel(tc, qh, kh, vh, Wo, bo, out):
         w_s = keep.tile([P, 2, D], U8, align_bytes=64)
         bias = keep.tile([P, D], BF16)
         qs_pad = keep.tile([P, H, P], BF16)
-        nc.vector.memset(qs_pad[:].bitcast(I32), 0)
+        nc.gpsimd.memset(qs_pad[:].bitcast(I32), 0)
         e_r = keep.tile([P, 2, NT, P], BF16)
         top_r = keep.tile([P, 2, 2], F32)
         shift_r = keep.tile([P, 2], F32)
@@ -191,6 +193,8 @@ def tile_sparseattention_pa_kernel(tc, qh, kh, vh, Wo, bo, out):
                 for j in range(j0, j0 + PACK):
                     nc.tensor.transpose(bank[:, j - j0, :], q_nat[:, j, :], ident[:])
                 nc.scalar.copy(out=q_t[:, j0 : j0 + PACK], in_=bank[:])
+                if j0 == 0:
+                    nc.scalar.copy(out=qs_pad[:, h, h % HG : P : HG], in_=q_t[:, 0, 0:P:PACK])
 
         def softmax(h):
             q_t, k_pad = q_ts[h], k_pads[h % N_KPAD]
@@ -236,7 +240,6 @@ def tile_sparseattention_pa_kernel(tc, qh, kh, vh, Wo, bo, out):
         def part_r_scores(h):
             hg, hl = divmod(h, HG)
             q_t, k_pad = q_ts[h], k_pads[h % N_KPAD]
-            nc.vector.tensor_copy(out=qs_pad[:, h, hl:P:HG], in_=q_t[:, 0, 0:P:PACK])
             for half in range(2):
                 if hl == 0:
                     r_banks[hg, half] = psum_o.tile([P, N_HALF], F32, tag="o_ps", name="r_ps%d" % half)
@@ -365,12 +368,13 @@ def tile_sparseattention_pa_kernel(tc, qh, kh, vh, Wo, bo, out):
                 part_r_scores(h - 2)
                 if h - 2 < N_EARLY:
                     part_b_operand(h - 2)
+            if h == 0:
+                strided_values()
             if 1 <= h <= H:
                 values(h - 1)
-        strided_values()
+            if h in (1, 2):
+                weights(h - 1)
         nc.sync.dma_start(out=bias[:], in_=bo.partition_broadcast(P))
-        for g in range(2):
-            weights(g)
         nc.vector.tensor_tensor(out=rsum[:], in0=rsum_a[:], in1=e_own[:], op=ALU.add)
         nc.vector.reciprocal(out=rinv[:], in_=rsum[:])
 
@@ -395,8 +399,11 @@ def tile_sparseattention_pa_kernel(tc, qh, kh, vh, Wo, bo, out):
         out_rows = out[0].rearrange("(p j) n -> p j n", j=NT)
         ctx_r_w = []
 
-        def query_tile(j):
+        tiles = {}
+
+        def attend(j):
             ctx_bf = stage.tile([P, H, DK], BF16, tag="ctx_bf")
+            tiles[j] = ctx_bf
             for hg in range(2):
                 heads = slice(hg * HG, (hg + 1) * HG)
                 c_ps = psum_f.tile([P, HG, DK], F32, tag="acc")
@@ -417,6 +424,9 @@ def tile_sparseattention_pa_kernel(tc, qh, kh, vh, Wo, bo, out):
                 for hl in range(HG):
                     h = hg * HG + hl
                     nc.scalar.activation(out=ctx_bf[:, h, :], in_=c_ps[:, hl, :], func=ACT.Copy, scale=rinv[:, h, j : j + 1])
+
+        def turn(j):
+            ctx_bf = tiles[j]
             bank = psum_t.tile([P, 2, 2, P], F32, tag="tp")
             for hg in range(2):
                 words = ctx_bf[:, hg * HG : (hg + 1) * HG, :].rearrange("p h d -> p (h d)").bitcast(F32)
@@ -441,6 +451,10 @@ def tile_sparseattention_pa_kernel(tc, qh, kh, vh, Wo, bo, out):
                 c_s[:].rearrange("p g q -> p (g q)"),
                 c_g[:].rearrange("p g q t -> p (g q t)"),
             )
+            tiles[j] = (c_c, c_s)
+
+        def project(j):
+            c_c, c_s = tiles[j]
             o_sb = stage.tile([P, D], F32, tag="o_sb", bufs=3)
             for nh in range(2):
                 cols = slice(nh * N_HALF, (nh + 1) * N_HALF)
@@ -493,9 +507,14 @@ def tile_sparseattention_pa_kernel(tc, qh, kh, vh, Wo, bo, out):
 
         order = list(range(1, NT)) + [0]
         part_b_tile(order[0])
-        for i, j in enumerate(order):
+        for i in range(NT + 2):
+            if i < NT:
+                attend(order[i])
             if i + 1 < NT:
                 part_b_tile(order[i + 1])
-            query_tile(j)
-            if i in (2, 3):
-                part_r(i - 2)
+            if 1 <= i <= NT:
+                turn(order[i - 1])
+            if i >= 2:
+                project(order[i - 2])
+            if i in (3, 4):
+                part_r(i - 3)

@@ -61,8 +61,20 @@ def tile_sparseattention_pa_kernel(tc, qh, kh, vh, Wo, bo, out):
         psum_f = ctx.enter_context(tc.psum_pool(name="psum_f", bufs=3))
         psum_o = ctx.enter_context(tc.psum_pool(name="psum_o", bufs=2))
 
+        ctx.enter_context(tc.manual_schedule())
+
         ident = const.tile([P, P], BF16)
         make_identity(nc, ident[:])
+
+        k_pads = [keep.tile([P, NT, NQ * K_STEP], BF16, name="k_pad%d" % i) for i in range(N_KPAD)]
+
+        def clear_gaps(k_pad):
+            runs = k_pad[:].rearrange("d j c -> d (j c)").bitcast(I32).rearrange("d (r c) -> d r c", c=K_STEP // 2)
+            nc.vector.memset(runs[:, :, NB // 2 :], 0)
+
+        clear_gaps(k_pads[0])
+        qs_pad = keep.tile([P, H, P], BF16)
+        nc.vector.memset(qs_pad[:].bitcast(I32), 0)
 
         mask_a32 = const.tile([P, NT, NB], F32)
         nc.gpsimd.memset(mask_a32[:], 0.0)
@@ -89,33 +101,31 @@ def tile_sparseattention_pa_kernel(tc, qh, kh, vh, Wo, bo, out):
             op0=ALU.add,
             op1=ALU.mult,
         )
-        k_pads = [keep.tile([P, NT, NQ * K_STEP], BF16, name="k_pad%d" % i) for i in range(N_KPAD)]
-        for i, k_pad in enumerate(k_pads):
-            engine = nc.vector if i == 0 else nc.gpsimd
-            engine.memset(k_pad[:].bitcast(I32), 0)
+        for k_pad in k_pads[1:]:
+            clear_gaps(k_pad)
 
-        mask_r32 = stage.tile([P, NT, NB, PACK], F32, tag="w_g", align_bytes=64)
+        mask_r32 = const.tile([P, NB, PACK], F32)
         nc.gpsimd.memset(mask_r32[:], 0.0)
         nc.gpsimd.affine_select(
             out=mask_r32[:],
             in_=mask_r32[:],
-            pattern=[[0, NT], [NB, NB], [0, PACK]],
+            pattern=[[NB, NB], [0, PACK]],
             compare_op=ALU.is_ge,
             fill=NEG,
             base=NB - 1,
             channel_multiplier=-8,
         )
-        nc.gpsimd.memset(mask_r32[:, 0, :, 0], 0.0)
-        mask_r = const.tile([P, S], BF16)
-        nc.gpsimd.tensor_scalar(
-            out=mask_r[:], in0=mask_r32[:].rearrange("r j a b -> r (j a b)"), scalar1=1.0, scalar2=0.0, op0=ALU.mult, op1=ALU.add
+        mask_r = const.tile([P, NT, P], BF16)
+        nc.vector.tensor_copy(
+            out=mask_r[:], in_=mask_r32[:].rearrange("r a b -> r (a b)").unsqueeze(1).to_broadcast([P, NT, P])
         )
+        nc.vector.memset(mask_r[:, 0, 0:P:PACK], 0.0)
 
         ident32 = const.tile([P, P], F32)
         nc.vector.tensor_copy(out=ident32[:], in_=ident[:])
 
         diag = const.tile([P, PACK, P, PACK], BF16)
-        nc.gpsimd.memset(diag[:].bitcast(I32), 0)
+        nc.vector.memset(diag[:].bitcast(I32), 0)
         for t in range(PACK):
             nc.vector.tensor_copy(out=diag[:, t, :, t], in_=ident[:])
 
@@ -143,7 +153,6 @@ def tile_sparseattention_pa_kernel(tc, qh, kh, vh, Wo, bo, out):
         rsum = keep.tile([P, H, NT], F32)
         rinv = keep.tile([P, H, NT], F32)
         e_pad = keep.tile([P, NT, PACK * P], BF16)
-        nc.gpsimd.memset(e_pad[:, :, H * NB : PACK * P].bitcast(I32), 0)
         ea_c = keep.tile([P, NT, P], U32, align_bytes=64)
         ea_s = keep.tile([P, NT, P], U8, align_bytes=64)
         eb_c = keep.tile([P, N_EARLY, NT, P], U32, align_bytes=64)
@@ -153,13 +162,12 @@ def tile_sparseattention_pa_kernel(tc, qh, kh, vh, Wo, bo, out):
         v_c = keep.tile([P, 2, H, DK], U32, align_bytes=64)
         v_s = keep.tile([P, 2, H, DK], U8, align_bytes=64)
         va_raw = keep.tile([P, PACK, DK], BF16)
+        va_w = keep.tile([P, DK, PACK], BF16)
         va_c = keep.tile([P, H, DK], U32, align_bytes=64)
         va_s = keep.tile([P, H, DK], U8, align_bytes=64)
         w_c = keep.tile([P, 2, D], U32, align_bytes=64)
         w_s = keep.tile([P, 2, D], U8, align_bytes=64)
         bias = keep.tile([P, D], BF16)
-        qs_pad = keep.tile([P, H, P], BF16)
-        nc.gpsimd.memset(qs_pad[:].bitcast(I32), 0)
         e_r = keep.tile([P, 2, NT, P], BF16)
         top_r = keep.tile([P, 2, 2], F32)
         shift_r = keep.tile([P, 2], F32)
@@ -169,36 +177,50 @@ def tile_sparseattention_pa_kernel(tc, qh, kh, vh, Wo, bo, out):
         er_c = keep.tile([P, 2, 2, P], U32, align_bytes=64)
         er_s = keep.tile([P, 2, 2, P], U8, align_bytes=64)
 
-        q_ts = {}
-        r_banks = {}
+        nats, q_ts, s_banks, r_banks, v_raws, v_gs, w_raws, w_gs, eb_gs = {}, {}, {}, {}, {}, {}, {}, {}, {}
 
-        def transposed(h):
-            k_nat = loads.tile([P, NT, DK], BF16, tag="k_nat")
-            nc.sync.dma_start(out=k_nat[:], in_=kh[0, h].rearrange("(p j) d -> p j d", j=NT))
-            q_nat = loads.tile([P, NT, DK], BF16, tag="q_nat")
-            nc.sync.dma_start(out=q_nat[:], in_=qh[0, h].rearrange("(p j) d -> p j d", j=NT))
-            q_t = loads.tile([P, NT, P], BF16, tag="q_t")
-            q_ts[h] = q_t
+        def load_kq(h):
+            for name, src in (("k_nat", kh), ("q_nat", qh)):
+                nat = loads.tile([P, NT, DK], BF16, tag=name, name=name)
+                nc.sync.dma_start(out=nat[:], in_=src[0, h].rearrange("(p j) d -> p j d", j=NT))
+                nats[name, h] = nat
+
+        def load_v(h):
+            v_raws[h] = loads.tile([P, 2, PACK, DK], BF16, tag="v_raw", name="v_raw")
+            nc.sync.dma_start(out=v_raws[h][:], in_=vh[0, h].rearrange("(p g t) d -> p g t d", g=2, t=PACK))
+
+        def load_w(g):
+            w_raws[g] = loads.tile([P, PACK, D], BF16, tag="w_raw", bufs=2, name="w_raw")
+            nc.sync.dma_start(
+                out=w_raws[g][:].rearrange("p (u e) n -> p u e n", u=2),
+                in_=Wo.rearrange("(g u p e) n -> g p u e n", g=2, u=2, e=2)[g],
+            )
+
+        def turn_keys(h):
             k_pad = k_pads[h % N_KPAD]
             for j0 in range(0, NT, PACK):
                 bank = psum_t.tile([P, PACK, P], BF16, tag="tp")
                 for j in range(j0, j0 + PACK):
-                    nc.tensor.transpose(bank[:, j - j0, :], k_nat[:, j, :], ident[:])
+                    nc.tensor.transpose(bank[:, j - j0, :], nats["k_nat", h][:, j, :], ident[:])
                 nc.scalar.copy(
                     out=k_pad[:, j0 : j0 + PACK].rearrange("d j (q c) -> d j q c", q=NQ)[:, :, :, 0:NB],
                     in_=bank[:].rearrange("d j (q c) -> d j q c", q=NQ),
                 )
+
+        def turn_queries(h):
+            q_t = loads.tile([P, NT, P], BF16, tag="q_t")
+            q_ts[h] = q_t
             for j0 in range(0, NT, PACK):
                 bank = psum_t.tile([P, PACK, P], BF16, tag="tp")
                 for j in range(j0, j0 + PACK):
-                    nc.tensor.transpose(bank[:, j - j0, :], q_nat[:, j, :], ident[:])
+                    nc.tensor.transpose(bank[:, j - j0, :], nats["q_nat", h][:, j, :], ident[:])
                 nc.scalar.copy(out=q_t[:, j0 : j0 + PACK], in_=bank[:])
-                if j0 == 0:
-                    nc.scalar.copy(out=qs_pad[:, h, h % HG : P : HG], in_=q_t[:, 0, 0:P:PACK])
+            nc.scalar.copy(out=qs_pad[:, h, h % HG : P : HG], in_=q_t[:, 0, 0:P:PACK])
 
-        def softmax(h):
+        def scores(h):
             q_t, k_pad = q_ts[h], k_pads[h % N_KPAD]
             s_ps = psum_f.tile([P, NT, 2, NB], F32, tag="acc")
+            s_banks[h] = s_ps
             nc.tensor.matmul(
                 out=s_ps[:].rearrange("p j i c -> p (j i c)"),
                 lhsT=ident[:],
@@ -222,29 +244,42 @@ def tile_sparseattention_pa_kernel(tc, qh, kh, vh, Wo, bo, out):
                         start=False,
                         stop=(j == NT - 1 and q == NQ - 1),
                     )
-            nc.vector.tensor_reduce(out=highs[:, h], in_=s_ps[:], axis=AXIS_X, op=ALU.max)
+
+        def find_highs(h):
+            nc.vector.tensor_reduce(out=highs[:, h], in_=s_banks[h][:], axis=AXIS_X, op=ALU.max)
+
+        def find_top(h):
             nc.vector.tensor_tensor(out=top[:, h], in0=highs[:, h, :, 0], in1=highs[:, h, :, 1], op=ALU.max)
+
+        def find_shifts(h):
             nc.vector.tensor_scalar(out=shift[:, h], in0=top[:, h], scalar1=-SCALE, scalar2=None, op0=ALU.mult)
             nc.vector.tensor_tensor(out=own_s[:, h], in0=highs[:, h, :, 1], in1=top[:, h], op=ALU.subtract)
+
+        def exps(h):
             nc.scalar.activation(out=e_own[:, h], in_=own_s[:, h], func=ACT.Exp, scale=SCALE)
             for j in range(NT):
                 nc.scalar.activation(
                     out=e_pad[:, j, h * NB : (h + 1) * NB],
-                    in_=s_ps[:, j, 0, :],
+                    in_=s_banks[h][:, j, 0, :],
                     func=ACT.Exp,
                     bias=shift[:, h, j : j + 1],
                     scale=SCALE,
                     accum_out=rsum_a[:, h, j : j + 1],
                 )
 
-        def part_r_scores(h):
+        def r_scores(h):
             hg, hl = divmod(h, HG)
-            q_t, k_pad = q_ts[h], k_pads[h % N_KPAD]
+            k_pad = k_pads[h % N_KPAD]
             for half in range(2):
                 if hl == 0:
                     r_banks[hg, half] = psum_o.tile([P, N_HALF], F32, tag="o_ps", name="r_ps%d" % half)
-                    cols = slice(half * N_HALF, (half + 1) * N_HALF)
-                    nc.tensor.matmul(out=r_banks[hg, half][:], lhsT=ident[:], rhs=mask_r[:, cols], start=True, stop=False)
+                    nc.tensor.matmul(
+                        out=r_banks[hg, half][:],
+                        lhsT=ident[:],
+                        rhs=mask_r[:, half * PACK : (half + 1) * PACK, :].rearrange("r j p -> r (j p)"),
+                        start=True,
+                        stop=False,
+                    )
                 nc.tensor.matmul(
                     out=r_banks[hg, half][:].rearrange("r (j q c) -> r j q c", j=PACK, q=NQ),
                     lhsT=qs_pad[:, h, :],
@@ -252,18 +287,24 @@ def tile_sparseattention_pa_kernel(tc, qh, kh, vh, Wo, bo, out):
                     start=False,
                     stop=(hl == HG - 1),
                 )
-            if hl < HG - 1:
-                return
+
+        def r_highs(hg):
             for half in range(2):
                 nc.vector.tensor_reduce(
                     out=top_r[:, hg, half : half + 1], in_=r_banks[hg, half][:], axis=AXIS_X, op=ALU.max
                 )
+
+        def r_top(hg):
             nc.vector.tensor_tensor(
                 out=shift_r[:, hg : hg + 1], in0=top_r[:, hg, 0:1], in1=top_r[:, hg, 1:2], op=ALU.max
             )
+
+        def r_shift(hg):
             nc.vector.tensor_scalar(
                 out=shift_r[:, hg : hg + 1], in0=shift_r[:, hg : hg + 1], scalar1=-SCALE, scalar2=None, op0=ALU.mult
             )
+
+        def r_exps(hg):
             for half in range(2):
                 nc.scalar.activation(
                     out=e_r[:, hg, half * PACK : (half + 1) * PACK, :].rearrange("r j p -> r (j p)"),
@@ -273,137 +314,121 @@ def tile_sparseattention_pa_kernel(tc, qh, kh, vh, Wo, bo, out):
                     scale=SCALE,
                     accum_out=rsum_r[:, hg, half : half + 1],
                 )
+
+        def r_sum(hg):
             nc.vector.tensor_tensor(
                 out=rinv_r[:, hg : hg + 1], in0=rsum_r[:, hg, 0:1], in1=rsum_r[:, hg, 1:2], op=ALU.add
             )
+
+        def r_inverse(hg):
             nc.vector.reciprocal(out=rinv_r[:, hg : hg + 1], in_=rinv_r[:, hg : hg + 1])
 
-        def part_b_operand(h):
-            eb_g = stage.tile([P, NT, P, PACK], BF16, tag="eb_g", align_bytes=64)
-            for j in range(NT):
-                nc.vector.tensor_scalar(
-                    out=eb_g[:, j].rearrange("p c t -> p (c t)"),
-                    in0=diag[:, j % PACK].rearrange("p c t -> p (c t)"),
-                    scalar1=e_own[:, h, j : j + 1],
-                    scalar2=None,
-                    op0=ALU.mult,
-                )
+        def fill(eb_g, slot, h, j):
+            nc.vector.tensor_scalar(
+                out=eb_g[:, slot].rearrange("p c t -> p (c t)"),
+                in0=diag[:, j % PACK].rearrange("p c t -> p (c t)"),
+                scalar1=e_own[:, h, j : j + 1],
+                scalar2=None,
+                op0=ALU.mult,
+            )
+
+        def head_fills(h):
+            eb_gs["head", h] = stage.tile([P, NT, P, PACK], BF16, tag="eb_g", align_bytes=64, name="eb_g")
+            return [lambda j=j: fill(eb_gs["head", h], j, h, j) for j in range(NT)]
+
+        def head_quantise(h):
             quantise(
                 nc,
                 eb_c[:, h].rearrange("p j c -> p (j c)"),
                 eb_s[:, h].rearrange("p j c -> p (j c)"),
-                eb_g[:].rearrange("p j c t -> p (j c t)"),
+                eb_gs["head", h][:].rearrange("p j c t -> p (j c t)"),
             )
 
-        def part_b_tile(j):
-            eb_g = stage.tile([P, H - N_EARLY, P, PACK], BF16, tag="eb_g", align_bytes=64)
-            for h in range(N_EARLY, H):
-                nc.vector.tensor_scalar(
-                    out=eb_g[:, h - N_EARLY].rearrange("p c t -> p (c t)"),
-                    in0=diag[:, j % PACK].rearrange("p c t -> p (c t)"),
-                    scalar1=e_own[:, h, j : j + 1],
-                    scalar2=None,
-                    op0=ALU.mult,
-                )
+        def tile_fills(j):
+            eb_gs["tile", j] = stage.tile([P, H - N_EARLY, P, PACK], BF16, tag="eb_g", align_bytes=64, name="eb_g")
+            return [lambda h=h: fill(eb_gs["tile", j], h - N_EARLY, h, j) for h in range(N_EARLY, H)]
+
+        def tile_quantise(j):
             quantise(
                 nc,
                 ebl_c[:, j].rearrange("p h c -> p (h c)"),
                 ebl_s[:, j].rearrange("p h c -> p (h c)"),
-                eb_g[:].rearrange("p h c t -> p (h c t)"),
+                eb_gs["tile", j][:].rearrange("p h c t -> p (h c t)"),
             )
 
-        def values(h):
-            v_raw = loads.tile([P, 2, PACK, DK], BF16, tag="v_raw")
-            nc.sync.dma_start(out=v_raw[:], in_=vh[0, h].rearrange("(p g t) d -> p g t d", g=2, t=PACK))
-            v_g = stage.tile([P, 2, DK, PACK], BF16, tag="v_g", align_bytes=64)
+        def v_regroup(h):
+            v_gs[h] = stage.tile([P, 2, DK, PACK], BF16, tag="v_g", align_bytes=64, name="v_g")
             for g in range(2):
                 nc.scalar.copy(
-                    out=v_g[:, g].rearrange("p (c i) t -> p c t i", i=4),
-                    in_=v_raw[:, g].rearrange("p t (c i) -> p c t i", i=4),
+                    out=v_gs[h][:, g].rearrange("p (c i) t -> p c t i", i=4),
+                    in_=v_raws[h][:, g].rearrange("p t (c i) -> p c t i", i=4),
                 )
-            for g in range(2):
-                quantise(nc, v_c[:, g, h, :], v_s[:, g, h, :], v_g[:, g].rearrange("p d t -> p (d t)"))
 
-        def strided_values():
-            nc.gpsimd.memset(va_raw[64:P], 0.0)
-            nc.sync.dma_start(
-                out=va_raw[0:64],
-                in_=vh[0].rearrange("h (x t s) d -> (h x) t s d", x=8, t=PACK)[:, :, 0, :],
-            )
-            va_w = keep.tile([P, DK, PACK], BF16)
-            va_g = stage.tile([P, H, DK, PACK], BF16, tag="eb_g", align_bytes=64)
+        def v_quantise(h):
+            for g in range(2):
+                quantise(nc, v_c[:, g, h, :], v_s[:, g, h, :], v_gs[h][:, g].rearrange("p d t -> p (d t)"))
+
+        va_gs = []
+
+        def va_regroup():
             nc.vector.tensor_copy(out=va_w[:], in_=va_raw[:].rearrange("p t d -> p d t"))
-            for h in range(H):
+
+        def va_spread():
+            va_gs.append(stage.tile([P, H, DK, PACK], BF16, tag="eb_g", align_bytes=64, name="va_g"))
+
+            def spread(h):
                 nc.vector.tensor_scalar(
-                    out=va_g[:, h], in0=va_w[:], scalar1=head_of[:, h : h + 1], scalar2=None, op0=ALU.mult
+                    out=va_gs[0][:, h], in0=va_w[:], scalar1=head_of[:, h : h + 1], scalar2=None, op0=ALU.mult
                 )
+
+            return [lambda h=h: spread(h) for h in range(H)]
+
+        def va_quantise():
             quantise(
                 nc,
                 va_c[:].rearrange("p h d -> p (h d)"),
                 va_s[:].rearrange("p h d -> p (h d)"),
-                va_g[:].rearrange("p h d t -> p (h d t)"),
+                va_gs[0][:].rearrange("p h d t -> p (h d t)"),
             )
 
-        def weights(g):
-            w_raw = loads.tile([P, PACK, D], BF16, tag="w_raw", bufs=2)
-            nc.sync.dma_start(
-                out=w_raw[:].rearrange("p (u e) n -> p u e n", u=2),
-                in_=Wo.rearrange("(g u p e) n -> g p u e n", g=2, u=2, e=2)[g],
+        def w_regroup(g, nh):
+            cols = slice(nh * N_HALF, (nh + 1) * N_HALF)
+            w_gs[g, nh] = stage.tile([P, N_HALF, PACK], BF16, tag="w_g", align_bytes=64, name="w_g")
+            nc.vector.tensor_copy(
+                out=w_gs[g, nh][:].rearrange("p (c i) t -> p c t i", i=4),
+                in_=w_raws[g][:, :, cols].rearrange("p t (c i) -> p c t i", i=4),
             )
-            for nh in range(2):
-                cols = slice(nh * N_HALF, (nh + 1) * N_HALF)
-                w_g = stage.tile([P, N_HALF, PACK], BF16, tag="w_g", align_bytes=64)
-                nc.vector.tensor_copy(
-                    out=w_g[:].rearrange("p (c i) t -> p c t i", i=4),
-                    in_=w_raw[:, :, cols].rearrange("p t (c i) -> p c t i", i=4),
-                )
-                quantise(nc, w_c[:, g, cols], w_s[:, g, cols], w_g[:].rearrange("p n t -> p (n t)"))
 
-        for h in range(H + 2):
-            if h < H:
-                transposed(h)
-            if 1 <= h <= H:
-                softmax(h - 1)
-            if h >= 2:
-                part_r_scores(h - 2)
-                if h - 2 < N_EARLY:
-                    part_b_operand(h - 2)
-            if h == 0:
-                strided_values()
-            if 1 <= h <= H:
-                values(h - 1)
-            if h in (1, 2):
-                weights(h - 1)
-        nc.sync.dma_start(out=bias[:], in_=bo.partition_broadcast(P))
-        nc.vector.tensor_tensor(out=rsum[:], in0=rsum_a[:], in1=e_own[:], op=ALU.add)
-        nc.vector.reciprocal(out=rinv[:], in_=rsum[:])
+        def w_quantise(g, nh):
+            cols = slice(nh * N_HALF, (nh + 1) * N_HALF)
+            quantise(nc, w_c[:, g, cols], w_s[:, g, cols], w_gs[g, nh][:].rearrange("p n t -> p (n t)"))
 
-        for j0 in range(0, NT, 2):
-            ea_g = stage.tile([P, 2, P, PACK], BF16, tag="ea_g", align_bytes=64)
+        out_rows = out[0].rearrange("(p j) n -> p j n", j=NT)
+        ea_gs, c_banks, ctx_bfs, c_gs, c_cs, o_banks, o_sbs = {}, {}, {}, {}, {}, {}, {}
+        er_gs, ctx_rs, picks, pickeds, rc_banks, ctx_r_ws = {}, {}, {}, {}, {}, {}
+
+        def turn_a(j0):
+            ea_gs[j0] = stage.tile([P, 2, P, PACK], BF16, tag="ea_g", align_bytes=64, name="ea_g")
             bank = psum_t.tile([P, 2, 2, P], F32, tag="tp")
             for j in range(j0, j0 + 2):
                 words = e_pad[:, j, :].bitcast(F32)
                 for u in range(2):
                     nc.tensor.transpose(bank[:, j - j0, u, :], words[:, u : 2 * P : 2], ident32[:])
             nc.scalar.copy(
-                out=ea_g[:].rearrange("p j q t -> p j (q t)").bitcast(F32).rearrange("p j (q u) -> p j q u", u=2),
+                out=ea_gs[j0][:].rearrange("p j q t -> p j (q t)").bitcast(F32).rearrange("p j (q u) -> p j q u", u=2),
                 in_=bank[:].rearrange("p j u q -> p j q u"),
             )
+
+        def quantise_a(j0):
             quantise(
                 nc,
                 ea_c[:, j0 : j0 + 2, :].rearrange("p j q -> p (j q)"),
                 ea_s[:, j0 : j0 + 2, :].rearrange("p j q -> p (j q)"),
-                ea_g[:].rearrange("p j q t -> p (j q t)"),
+                ea_gs[j0][:].rearrange("p j q t -> p (j q t)"),
             )
 
-        out_rows = out[0].rearrange("(p j) n -> p j n", j=NT)
-        ctx_r_w = []
-
-        tiles = {}
-
         def attend(j):
-            ctx_bf = stage.tile([P, H, DK], BF16, tag="ctx_bf")
-            tiles[j] = ctx_bf
+            ctx_bfs[j] = stage.tile([P, H, DK], BF16, tag="ctx_bf", name="ctx_bf")
             for hg in range(2):
                 heads = slice(hg * HG, (hg + 1) * HG)
                 c_ps = psum_f.tile([P, HG, DK], F32, tag="acc")
@@ -423,17 +448,16 @@ def tile_sparseattention_pa_kernel(tc, qh, kh, vh, Wo, bo, out):
                     )
                 for hl in range(HG):
                     h = hg * HG + hl
-                    nc.scalar.activation(out=ctx_bf[:, h, :], in_=c_ps[:, hl, :], func=ACT.Copy, scale=rinv[:, h, j : j + 1])
+                    nc.scalar.activation(out=ctx_bfs[j][:, h, :], in_=c_ps[:, hl, :], func=ACT.Copy, scale=rinv[:, h, j : j + 1])
 
-        def turn(j):
-            ctx_bf = tiles[j]
+        def turn_ctx(j):
             bank = psum_t.tile([P, 2, 2, P], F32, tag="tp")
             for hg in range(2):
-                words = ctx_bf[:, hg * HG : (hg + 1) * HG, :].rearrange("p h d -> p (h d)").bitcast(F32)
+                words = ctx_bfs[j][:, hg * HG : (hg + 1) * HG, :].rearrange("p h d -> p (h d)").bitcast(F32)
                 for u in range(2):
                     nc.tensor.transpose(bank[:, hg, u, :], words[:, u * P : (u + 1) * P], ident32[:])
-            c_g = stage.tile([P, 2, P, PACK], BF16, tag="c_g", align_bytes=64)
-            c_gw = c_g[:].rearrange("p g q t -> p (g q t)").bitcast(F32).rearrange("p (g q u) -> p g q u", g=2, u=2)
+            c_gs[j] = stage.tile([P, 2, P, PACK], BF16, tag="c_g", align_bytes=64, name="c_g")
+            c_gw = c_gs[j][:].rearrange("p g q t -> p (g q t)").bitcast(F32).rearrange("p (g q u) -> p g q u", g=2, u=2)
             nc.scalar.copy(out=c_gw, in_=bank[:].rearrange("p g u q -> p g q u"))
             if j == 0:
                 for hg in range(2):
@@ -441,42 +465,57 @@ def tile_sparseattention_pa_kernel(tc, qh, kh, vh, Wo, bo, out):
                         rows = slice(64 * f, 64 * (f + 1))
                         nc.scalar.copy(
                             out=c_gw[rows, hg, 0:P:PACK, :],
-                            in_=ctx_r_w[hg][rows].rearrange("d (a u f) -> d a u f", u=2, f=2)[:, :, :, f],
+                            in_=ctx_r_ws[hg][rows].rearrange("d (a u f) -> d a u f", u=2, f=2)[:, :, :, f],
                         )
+
+        def quantise_ctx(j):
             c_c = stage.tile([P, 2, P], U32, tag="c_c", align_bytes=64)
             c_s = stage.tile([P, 2, P], U8, tag="c_s", align_bytes=64)
+            c_cs[j] = (c_c, c_s)
             quantise(
                 nc,
                 c_c[:].rearrange("p g q -> p (g q)"),
                 c_s[:].rearrange("p g q -> p (g q)"),
-                c_g[:].rearrange("p g q t -> p (g q t)"),
+                c_gs[j][:].rearrange("p g q t -> p (g q t)"),
             )
-            tiles[j] = (c_c, c_s)
 
         def project(j):
-            c_c, c_s = tiles[j]
-            o_sb = stage.tile([P, D], F32, tag="o_sb", bufs=3)
+            c_c, c_s = c_cs[j]
             for nh in range(2):
                 cols = slice(nh * N_HALF, (nh + 1) * N_HALF)
-                o_ps = psum_o.tile([P, N_HALF], F32, tag="o_ps")
+                o_banks[j, nh] = psum_o.tile([P, N_HALF], F32, tag="o_ps", name="o_ps")
                 for g in range(2):
-                    mx_pass(nc, o_ps[:], c_c[:, g, :], c_s[:, g, :], w_c[:, g, cols], w_s[:, g, cols], g == 0, g == 1)
-                nc.vector.tensor_tensor(out=o_sb[:, cols], in0=o_ps[:], in1=bias[:, cols], op=ALU.add)
-            nc.sync.dma_start(out=out_rows[:, j, :], in_=o_sb[:])
+                    mx_pass(
+                        nc, o_banks[j, nh][:], c_c[:, g, :], c_s[:, g, :], w_c[:, g, cols], w_s[:, g, cols], g == 0, g == 1
+                    )
 
-        def part_r(hg):
+        def add_bias(j, nh):
+            if nh == 0:
+                o_sbs[j] = stage.tile([P, D], F32, tag="o_sb", bufs=3, name="o_sb")
+            cols = slice(nh * N_HALF, (nh + 1) * N_HALF)
+            nc.vector.tensor_tensor(out=o_sbs[j][:, cols], in0=o_banks[j, nh][:], in1=bias[:, cols], op=ALU.add)
+
+        def store(j):
+            nc.sync.dma_start(out=out_rows[:, j, :], in_=o_sbs[j][:])
+
+        def r_turn(hg):
             for g in range(2):
                 bank = psum_t.tile([P, PACK, P], BF16, tag="tp")
                 for t in range(PACK):
                     nc.tensor.transpose(bank[:, t, :], e_r[:, hg, g * PACK + t, :], ident[:])
                 nc.scalar.copy(out=er_g[:, hg, g], in_=bank[:].rearrange("p t r -> p r t"))
+
+        def r_quantise(hg):
             quantise(
                 nc,
                 er_c[:, hg].rearrange("p g r -> p (g r)"),
                 er_s[:, hg].rearrange("p g r -> p (g r)"),
                 er_g[:, hg].rearrange("p g r t -> p (g r t)"),
             )
+
+        def r_attend(hg):
             rc_ps = psum_f.tile([P, HG, DK], F32, tag="acc")
+            rc_banks[hg] = rc_ps
             heads = slice(hg * HG, (hg + 1) * HG)
             for g in range(2):
                 mx_pass(
@@ -489,32 +528,160 @@ def tile_sparseattention_pa_kernel(tc, qh, kh, vh, Wo, bo, out):
                     start=(g == 0),
                     stop=(g == 1),
                 )
-            pick = stage.tile([P, HG], F32, tag="pick")
+
+        def r_factors(hg):
+            picks[hg] = stage.tile([P, HG], F32, tag="pick", name="pick")
             nc.vector.tensor_scalar(
-                out=pick[:], in0=own_head[:], scalar1=rinv_r[:, hg : hg + 1], scalar2=None, op0=ALU.mult
+                out=picks[hg][:], in0=own_head[:], scalar1=rinv_r[:, hg : hg + 1], scalar2=None, op0=ALU.mult
             )
-            picked = stage.tile([P, HG, DK], F32, tag="picked")
+
+        def r_pick(hg):
+            pickeds[hg] = stage.tile([P, HG, DK], F32, tag="picked", name="picked")
             nc.vector.tensor_tensor(
-                out=picked[:], in0=rc_ps[:], in1=pick[:].unsqueeze(2).to_broadcast([P, HG, DK]), op=ALU.mult
+                out=pickeds[hg][:],
+                in0=rc_banks[hg][:],
+                in1=picks[hg][:].unsqueeze(2).to_broadcast([P, HG, DK]),
+                op=ALU.mult,
             )
-            ctx_r = stage.tile([P, 2, DK], BF16, tag="ctx_r")
-            nc.vector.tensor_tensor(out=ctx_r[:], in0=picked[:, 0:2, :], in1=picked[:, 2:4, :], op=ALU.add)
+
+        def r_join(hg):
+            ctx_rs[hg] = stage.tile([P, 2, DK], BF16, tag="ctx_r", name="ctx_r")
+            nc.vector.tensor_tensor(
+                out=ctx_rs[hg][:], in0=pickeds[hg][:, 0:2, :], in1=pickeds[hg][:, 2:4, :], op=ALU.add
+            )
+
+        def r_turn_ctx(hg):
             bank = psum_t.tile([P, P], F32, tag="tp")
-            nc.tensor.transpose(bank[:], ctx_r[:].rearrange("r f d -> r (f d)").bitcast(F32), ident32[:])
-            ctx_w = keep.tile([P, P], F32, name="ctx_r_w%d" % hg)
-            nc.scalar.copy(out=ctx_w[:], in_=bank[:])
-            ctx_r_w.append(ctx_w)
+            nc.tensor.transpose(bank[:], ctx_rs[hg][:].rearrange("r f d -> r (f d)").bitcast(F32), ident32[:])
+            ctx_r_ws[hg] = keep.tile([P, P], F32, name="ctx_r_w%d" % hg)
+            nc.scalar.copy(out=ctx_r_ws[hg][:], in_=bank[:])
+
+        def weave(chain, fillers):
+            n = len(chain) + 1
+            for i in range(n):
+                for f in fillers[i * len(fillers) // n : (i + 1) * len(fillers) // n]:
+                    f()
+                if i < len(chain):
+                    chain[i]()
+
+        load_kq(0)
+        nc.vector.memset(va_raw[64:P].rearrange("p t d -> p (t d)").bitcast(I32), 0)
+        nc.sync.dma_start(
+            out=va_raw[0:64],
+            in_=vh[0].rearrange("h (x t s) d -> (h x) t s d", x=8, t=PACK)[:, :, 0, :],
+        )
+        load_kq(1)
+        load_v(0)
+        w_units = [(g, nh) for g in range(2) for nh in range(2)]
+        for s in range(H + 2):
+            if s + 2 < H:
+                load_kq(s + 2)
+            if s + 1 < H:
+                load_v(s + 1)
+            if s in (2, 3):
+                load_w(s - 2)
+            if s == 4:
+                nc.sync.dma_start(out=bias[:], in_=bo.partition_broadcast(P))
+            r_done = [hg for hg in range(2) if s == HG * hg + HG + 1]
+            r_ready = [hg for hg in range(2) if s == HG * hg + HG + 2]
+
+            if s < H:
+                turn_keys(s)
+            for hg in r_ready:
+                r_exps(hg)
+            if 1 <= s <= H:
+                scores(s - 1)
+            if s >= 2:
+                exps(s - 2)
+            if s < H:
+                turn_queries(s)
+            if s >= 2:
+                r_scores(s - 2)
+            if s == HG + 3:
+                r_turn(0)
+            if 1 <= s <= H:
+                v_regroup(s - 1)
+            if s == HG + 5:
+                r_attend(0)
+
+            fillers, behind = [], []
+            if s == 1:
+                fillers += [va_regroup] + va_spread()
+                behind += [va_quantise]
+            if s == 2:
+                fillers += [lambda: nc.vector.memset(e_pad[:, :, H * NB : PACK * P].bitcast(I32), 0)]
+            if s >= 2:
+                fillers += [lambda h=s - 2: v_quantise(h)]
+            if 3 <= s < N_EARLY + 3:
+                fillers += head_fills(s - 3)
+                behind += [lambda h=s - 3: head_quantise(h)]
+            if s >= N_EARLY + 2:
+                unit = w_units[s - N_EARLY - 2]
+                fillers += [lambda u=unit: w_regroup(*u)]
+                behind += [lambda u=unit: w_quantise(*u)]
+            if s == HG + 3:
+                fillers += [lambda: r_sum(0)]
+            if s == HG + 4:
+                fillers += [lambda: r_inverse(0), lambda: r_quantise(0)]
+            if s == HG + 5:
+                fillers += [lambda: r_factors(0)]
+            chain = []
+            if 1 <= s <= H:
+                chain += [lambda: find_highs(s - 1), lambda: find_top(s - 1), lambda: find_shifts(s - 1)]
+            weave(chain, fillers)
+            chain = []
+            for hg in r_done:
+                chain += [lambda: r_highs(hg), lambda: r_top(hg), lambda: r_shift(hg)]
+            weave(chain, behind)
 
         order = list(range(1, NT)) + [0]
-        part_b_tile(order[0])
-        for i in range(NT + 2):
+        fills = tile_fills(order[0])
+        for j0 in range(0, NT, 2):
+            turn_a(j0)
+        r_exps(1)
+        nc.vector.tensor_tensor(out=rsum[:], in0=rsum_a[:], in1=e_own[:], op=ALU.add)
+        for f in fills:
+            f()
+        nc.vector.reciprocal(out=rinv[:], in_=rsum[:])
+        r_pick(0)
+        tile_quantise(order[0])
+        for j0 in range(0, NT, 2):
+            quantise_a(j0)
+        r_sum(1)
+        r_join(0)
+        for i in range(NT + 3):
             if i < NT:
                 attend(order[i])
-            if i + 1 < NT:
-                part_b_tile(order[i + 1])
+            if i == 1:
+                r_turn_ctx(0)
+            if i == 6:
+                r_turn_ctx(1)
             if 1 <= i <= NT:
-                turn(order[i - 1])
-            if i >= 2:
+                turn_ctx(order[i - 1])
+            if 2 <= i <= NT + 1:
                 project(order[i - 2])
-            if i in (3, 4):
-                part_r(i - 3)
+            if i == 2:
+                r_turn(1)
+            if i == 4:
+                r_attend(1)
+            if i + 1 < NT:
+                for f in tile_fills(order[i + 1]):
+                    f()
+            if i == 2:
+                r_inverse(1)
+            if i >= 3:
+                add_bias(order[i - 3], 1)
+                store(order[i - 3])
+            if i + 1 < NT:
+                tile_quantise(order[i + 1])
+            if i == 3:
+                r_quantise(1)
+                r_factors(1)
+            if i == 5:
+                r_pick(1)
+            if 1 <= i <= NT:
+                quantise_ctx(order[i - 1])
+            if i == 5:
+                r_join(1)
+            if 2 <= i <= NT + 1:
+                add_bias(order[i - 2], 0)

@@ -68,11 +68,15 @@ def tile_sparseattention_pa_kernel(tc, qh, kh, vh, Wo, bo, out):
 
         k_pads = [keep.tile([P, NT, NQ * K_STEP], BF16, name="k_pad%d" % i) for i in range(N_KPAD)]
 
-        def clear_gaps(k_pad):
-            runs = k_pad[:].rearrange("d j c -> d (j c)").bitcast(I32).rearrange("d (r c) -> d r c", c=K_STEP // 2)
-            nc.vector.memset(runs[:, :, NB // 2 :], 0)
-
-        clear_gaps(k_pads[0])
+        runs = [
+            k_pad[:].rearrange("d j c -> d (j c)").bitcast(F32).rearrange("d (r c) -> d r c", c=K_STEP // 2)[:, :, NB // 2 :]
+            for k_pad in k_pads
+        ]
+        n_gap = (K_STEP - NB) // 2
+        zero = const.tile([P, n_gap], F32)
+        nc.vector.memset(zero[:], 0.0)
+        nc.vector.memset(runs[0].bitcast(I32), 0)
+        nc.scalar.copy(out=runs[1], in_=zero[:].unsqueeze(1).to_broadcast([P, NT * NQ, n_gap]))
         qs_pad = keep.tile([P, H, P], BF16)
         nc.vector.memset(qs_pad[:].bitcast(I32), 0)
 
@@ -101,9 +105,6 @@ def tile_sparseattention_pa_kernel(tc, qh, kh, vh, Wo, bo, out):
             op0=ALU.add,
             op1=ALU.mult,
         )
-        for k_pad in k_pads[1:]:
-            clear_gaps(k_pad)
-
         mask_r32 = const.tile([P, NB, PACK], F32)
         nc.gpsimd.memset(mask_r32[:], 0.0)
         nc.gpsimd.affine_select(
@@ -115,6 +116,7 @@ def tile_sparseattention_pa_kernel(tc, qh, kh, vh, Wo, bo, out):
             base=NB - 1,
             channel_multiplier=-8,
         )
+        nc.gpsimd.memset(runs[2].bitcast(I32), 0)
         mask_r = const.tile([P, NT, P], BF16)
         nc.vector.tensor_copy(
             out=mask_r[:], in_=mask_r32[:].rearrange("r a b -> r (a b)").unsqueeze(1).to_broadcast([P, NT, P])
@@ -495,8 +497,9 @@ def tile_sparseattention_pa_kernel(tc, qh, kh, vh, Wo, bo, out):
             cols = slice(nh * N_HALF, (nh + 1) * N_HALF)
             nc.vector.tensor_tensor(out=o_sbs[j][:, cols], in0=o_banks[j, nh][:], in1=bias[:, cols], op=ALU.add)
 
-        def store(j):
-            nc.sync.dma_start(out=out_rows[:, j, :], in_=o_sbs[j][:])
+        def store(j, nh):
+            cols = slice(nh * N_HALF, (nh + 1) * N_HALF)
+            nc.sync.dma_start(out=out_rows[:, j, cols], in_=o_sbs[j][:, cols])
 
         def r_turn(hg):
             for g in range(2):
@@ -573,6 +576,7 @@ def tile_sparseattention_pa_kernel(tc, qh, kh, vh, Wo, bo, out):
         load_kq(1)
         load_v(0)
         w_units = [(g, nh) for g in range(2) for nh in range(2)]
+        behind = []
         for s in range(H + 2):
             if s + 2 < H:
                 load_kq(s + 2)
@@ -604,18 +608,18 @@ def tile_sparseattention_pa_kernel(tc, qh, kh, vh, Wo, bo, out):
             if s == HG + 5:
                 r_attend(0)
 
-            fillers, behind = [], []
+            fillers, behind = behind, []
             if s == 1:
-                fillers += [va_regroup] + va_spread()
-                behind += [va_quantise]
-            if s == 2:
+                fillers += [va_regroup]
                 fillers += [lambda: nc.vector.memset(e_pad[:, :, H * NB : PACK * P].bitcast(I32), 0)]
+                fillers += va_spread()
+                behind += [va_quantise]
             if s >= 2:
-                fillers += [lambda h=s - 2: v_quantise(h)]
+                fillers = [lambda h=s - 2: v_quantise(h)] + fillers
             if 3 <= s < N_EARLY + 3:
                 fillers += head_fills(s - 3)
                 behind += [lambda h=s - 3: head_quantise(h)]
-            if s >= N_EARLY + 2:
+            if N_EARLY + 2 <= s < N_EARLY + 5:
                 unit = w_units[s - N_EARLY - 2]
                 fillers += [lambda u=unit: w_regroup(*u)]
                 behind += [lambda u=unit: w_quantise(*u)]
@@ -628,60 +632,66 @@ def tile_sparseattention_pa_kernel(tc, qh, kh, vh, Wo, bo, out):
             chain = []
             if 1 <= s <= H:
                 chain += [lambda: find_highs(s - 1), lambda: find_top(s - 1), lambda: find_shifts(s - 1)]
-            weave(chain, fillers)
-            chain = []
             for hg in r_done:
                 chain += [lambda: r_highs(hg), lambda: r_top(hg), lambda: r_shift(hg)]
-            weave(chain, behind)
+            weave(chain, fillers)
 
-        order = list(range(1, NT)) + [0]
+        order = [1, 2, 3, 4, 5, 0, 6, 7]
         fills = tile_fills(order[0])
         for j0 in range(0, NT, 2):
             turn_a(j0)
         r_exps(1)
+        for f in behind:
+            f()
         nc.vector.tensor_tensor(out=rsum[:], in0=rsum_a[:], in1=e_own[:], op=ALU.add)
         for f in fills:
             f()
         nc.vector.reciprocal(out=rinv[:], in_=rsum[:])
-        r_pick(0)
+        quantise_a(0)
         tile_quantise(order[0])
-        for j0 in range(0, NT, 2):
+        for j0 in range(2, NT, 2):
             quantise_a(j0)
         r_sum(1)
-        r_join(0)
+        w_regroup(*w_units[3])
+        r_inverse(1)
         for i in range(NT + 3):
             if i < NT:
                 attend(order[i])
-            if i == 1:
+            if i == 3:
                 r_turn_ctx(0)
-            if i == 6:
+            if i == 5:
                 r_turn_ctx(1)
             if 1 <= i <= NT:
                 turn_ctx(order[i - 1])
             if 2 <= i <= NT + 1:
                 project(order[i - 2])
-            if i == 2:
+            if i == 0:
                 r_turn(1)
-            if i == 4:
+            if i == 2:
                 r_attend(1)
             if i + 1 < NT:
                 for f in tile_fills(order[i + 1]):
                     f()
-            if i == 2:
-                r_inverse(1)
-            if i >= 3:
-                add_bias(order[i - 3], 1)
-                store(order[i - 3])
-            if i + 1 < NT:
-                tile_quantise(order[i + 1])
-            if i == 3:
+            if i == 0:
+                w_quantise(*w_units[3])
+            if i == 1:
                 r_quantise(1)
                 r_factors(1)
-            if i == 5:
+            if i == 2:
+                r_pick(0)
+            if i == 3:
                 r_pick(1)
+            if i >= 3:
+                add_bias(order[i - 3], 1)
+                store(order[i - 3], 1)
+            if i + 1 < NT:
+                tile_quantise(order[i + 1])
+            if i == 2:
+                r_join(0)
+            if i == 3:
+                r_join(1)
             if 1 <= i <= NT:
                 quantise_ctx(order[i - 1])
-            if i == 5:
-                r_join(1)
             if 2 <= i <= NT + 1:
                 add_bias(order[i - 2], 0)
+                store(order[i - 2], 0)

@@ -75,11 +75,16 @@ def tile_sparseattention_pa_kernel(tc, qh, kh, vh, Wo, bo, out):
         n_gap = (K_STEP - NB) // 2
         zero = const.tile([P, n_gap], F32)
         nc.vector.memset(zero[:], 0.0)
+        one = const.tile([P, 1], F32)
+        nc.scalar.activation(out=one[:], in_=zero[:, 0:1], func=ACT.Exp)
         nc.vector.memset(runs[0].bitcast(I32), 0)
         nc.scalar.copy(out=runs[1], in_=zero[:].unsqueeze(1).to_broadcast([P, NT * NQ, n_gap]))
         qs_pad = keep.tile([P, H, P], BF16)
         nc.vector.memset(qs_pad[:].bitcast(I32), 0)
 
+        n_diag = PACK * P
+        diag = const.tile([P, PACK * (n_diag + 1)], BF16)
+        nc.vector.memset(diag[:].bitcast(I32), 0)
         mask_a32 = const.tile([P, NT, NB], F32)
         nc.gpsimd.memset(mask_a32[:], 0.0)
         nc.gpsimd.affine_select(
@@ -118,33 +123,42 @@ def tile_sparseattention_pa_kernel(tc, qh, kh, vh, Wo, bo, out):
         )
         nc.gpsimd.memset(runs[2].bitcast(I32), 0)
         mask_r = const.tile([P, NT, P], BF16)
-        nc.vector.tensor_copy(
-            out=mask_r[:], in_=mask_r32[:].rearrange("r a b -> r (a b)").unsqueeze(1).to_broadcast([P, NT, P])
-        )
-        nc.vector.memset(mask_r[:, 0, 0:P:PACK], 0.0)
-
         ident32 = const.tile([P, P], F32)
-        nc.vector.tensor_copy(out=ident32[:], in_=ident[:])
-
-        diag = const.tile([P, PACK, P, PACK], BF16)
-        nc.vector.memset(diag[:].bitcast(I32), 0)
-        for t in range(PACK):
-            nc.vector.tensor_copy(out=diag[:, t, :, t], in_=ident[:])
-
         head_of = const.tile([P, H], F32)
-        nc.vector.tensor_reduce(
-            out=head_of[:],
-            in_=ident[:, 0 : H * 8].rearrange("p (h x) -> p h x", x=8),
-            axis=AXIS_X,
-            op=ALU.add,
-        )
         own_head = const.tile([P, HG], F32)
-        nc.vector.tensor_reduce(
-            out=own_head[:],
-            in_=ident[:].rearrange("p (a h) -> p h a", h=HG),
-            axis=AXIS_X,
-            op=ALU.add,
-        )
+
+        def make_mask_r():
+            nc.vector.tensor_copy(
+                out=mask_r[:], in_=mask_r32[:].rearrange("r a b -> r (a b)").unsqueeze(1).to_broadcast([P, NT, P])
+            )
+
+        def open_mask_r():
+            nc.vector.memset(mask_r[:, 0, 0:P:PACK], 0.0)
+
+        def make_ident32():
+            nc.vector.tensor_copy(out=ident32[:], in_=ident[:])
+
+        def make_diag():
+            nc.vector.tensor_copy(
+                out=diag[:].rearrange("p (t x) -> p t x", t=PACK)[:, :, 0:n_diag:PACK],
+                in_=ident[:].unsqueeze(1).to_broadcast([P, PACK, P]),
+            )
+
+        def make_head_of():
+            nc.vector.tensor_reduce(
+                out=head_of[:],
+                in_=ident[:, 0 : H * 8].rearrange("p (h x) -> p h x", x=8),
+                axis=AXIS_X,
+                op=ALU.add,
+            )
+
+        def make_own_head():
+            nc.vector.tensor_reduce(
+                out=own_head[:],
+                in_=ident[:].rearrange("p (a h) -> p h a", h=HG),
+                axis=AXIS_X,
+                op=ALU.add,
+            )
 
         highs = keep.tile([P, H, NT, 2], F32)
         top = keep.tile([P, H, NT], F32)
@@ -161,8 +175,8 @@ def tile_sparseattention_pa_kernel(tc, qh, kh, vh, Wo, bo, out):
         eb_s = keep.tile([P, N_EARLY, NT, P], U8, align_bytes=64)
         ebl_c = keep.tile([P, NT, H - N_EARLY, P], U32, align_bytes=64)
         ebl_s = keep.tile([P, NT, H - N_EARLY, P], U8, align_bytes=64)
-        v_c = keep.tile([P, 2, H, DK], U32, align_bytes=64)
-        v_s = keep.tile([P, 2, H, DK], U8, align_bytes=64)
+        v_c = keep.tile([P, H, 2, DK], U32, align_bytes=64)
+        v_s = keep.tile([P, H, 2, DK], U8, align_bytes=64)
         va_raw = keep.tile([P, PACK, DK], BF16)
         va_w = keep.tile([P, DK, PACK], BF16)
         va_c = keep.tile([P, H, DK], U32, align_bytes=64)
@@ -170,7 +184,7 @@ def tile_sparseattention_pa_kernel(tc, qh, kh, vh, Wo, bo, out):
         w_c = keep.tile([P, 2, D], U32, align_bytes=64)
         w_s = keep.tile([P, 2, D], U8, align_bytes=64)
         bias = keep.tile([P, D], BF16)
-        e_r = keep.tile([P, 2, NT, P], BF16)
+        e_r = keep.tile([P, 2, 2, P, PACK], BF16)
         top_r = keep.tile([P, 2, 2], F32)
         shift_r = keep.tile([P, 2], F32)
         rsum_r = keep.tile([P, 2, 2], F32)
@@ -254,8 +268,8 @@ def tile_sparseattention_pa_kernel(tc, qh, kh, vh, Wo, bo, out):
             nc.vector.tensor_tensor(out=top[:, h], in0=highs[:, h, :, 0], in1=highs[:, h, :, 1], op=ALU.max)
 
         def find_shifts(h):
-            nc.vector.tensor_scalar(out=shift[:, h], in0=top[:, h], scalar1=-SCALE, scalar2=None, op0=ALU.mult)
-            nc.vector.tensor_tensor(out=own_s[:, h], in0=highs[:, h, :, 1], in1=top[:, h], op=ALU.subtract)
+            nc.gpsimd.tensor_tensor(out=own_s[:, h], in0=highs[:, h, :, 1], in1=top[:, h], op=ALU.subtract)
+            nc.gpsimd.tensor_scalar(out=shift[:, h], in0=top[:, h], scalar1=-SCALE, scalar2=0.0, op0=ALU.mult, op1=ALU.add)
 
         def exps(h):
             nc.scalar.activation(out=e_own[:, h], in_=own_s[:, h], func=ACT.Exp, scale=SCALE)
@@ -309,8 +323,8 @@ def tile_sparseattention_pa_kernel(tc, qh, kh, vh, Wo, bo, out):
         def r_exps(hg):
             for half in range(2):
                 nc.scalar.activation(
-                    out=e_r[:, hg, half * PACK : (half + 1) * PACK, :].rearrange("r j p -> r (j p)"),
-                    in_=r_banks[hg, half][:],
+                    out=e_r[:, hg, half],
+                    in_=r_banks[hg, half][:].rearrange("r (t p) -> r p t", t=PACK),
                     func=ACT.Exp,
                     bias=shift_r[:, hg : hg + 1],
                     scale=SCALE,
@@ -328,7 +342,7 @@ def tile_sparseattention_pa_kernel(tc, qh, kh, vh, Wo, bo, out):
         def fill(eb_g, slot, h, j):
             nc.vector.tensor_scalar(
                 out=eb_g[:, slot].rearrange("p c t -> p (c t)"),
-                in0=diag[:, j % PACK].rearrange("p c t -> p (c t)"),
+                in0=diag[:, j % PACK * n_diag : (j % PACK + 1) * n_diag],
                 scalar1=e_own[:, h, j : j + 1],
                 scalar2=None,
                 op0=ALU.mult,
@@ -367,8 +381,12 @@ def tile_sparseattention_pa_kernel(tc, qh, kh, vh, Wo, bo, out):
                 )
 
         def v_quantise(h):
-            for g in range(2):
-                quantise(nc, v_c[:, g, h, :], v_s[:, g, h, :], v_gs[h][:, g].rearrange("p d t -> p (d t)"))
+            quantise(
+                nc,
+                v_c[:, h].rearrange("p g d -> p (g d)"),
+                v_s[:, h].rearrange("p g d -> p (g d)"),
+                v_gs[h][:].rearrange("p g d t -> p (g d t)"),
+            )
 
         va_gs = []
 
@@ -401,6 +419,13 @@ def tile_sparseattention_pa_kernel(tc, qh, kh, vh, Wo, bo, out):
                 in_=w_raws[g][:, :, cols].rearrange("p t (c i) -> p c t i", i=4),
             )
 
+        def w_regroup_on_scalar(g, nh):
+            w_gs[g, nh] = stage.tile([P, N_HALF, PACK], BF16, tag="w_g", align_bytes=64, name="w_g")
+            nc.scalar.copy(
+                out=w_gs[g, nh][:].rearrange("p (c i) t -> p c t i", i=4),
+                in_=w_raws[g][:, :, nh * N_HALF : (nh + 1) * N_HALF].rearrange("p t (c i) -> p c t i", i=4),
+            )
+
         def w_quantise(g, nh):
             cols = slice(nh * N_HALF, (nh + 1) * N_HALF)
             quantise(nc, w_c[:, g, cols], w_s[:, g, cols], w_gs[g, nh][:].rearrange("p n t -> p (n t)"))
@@ -429,7 +454,7 @@ def tile_sparseattention_pa_kernel(tc, qh, kh, vh, Wo, bo, out):
                 ea_gs[j0][:].rearrange("p j q t -> p (j q t)"),
             )
 
-        def attend(j):
+        def attend(j, on_vector):
             ctx_bfs[j] = stage.tile([P, H, DK], BF16, tag="ctx_bf", name="ctx_bf")
             for hg in range(2):
                 heads = slice(hg * HG, (hg + 1) * HG)
@@ -446,8 +471,16 @@ def tile_sparseattention_pa_kernel(tc, qh, kh, vh, Wo, bo, out):
                         e_codes, e_scales = ebl_c[:, j, h - N_EARLY, :], ebl_s[:, j, h - N_EARLY, :]
                     mx_pass(
                         nc, c_ps[:, hl, :], e_codes, e_scales,
-                        v_c[:, j // PACK, h, :], v_s[:, j // PACK, h, :], False, hl == HG - 1,
+                        v_c[:, h, j // PACK, :], v_s[:, h, j // PACK, :], False, hl == HG - 1,
                     )
+                if hg == 1 and on_vector:
+                    nc.vector.tensor_tensor(
+                        out=ctx_bfs[j][:, heads],
+                        in0=c_ps[:],
+                        in1=rinv[:, heads, j].unsqueeze(2).to_broadcast([P, HG, DK]),
+                        op=ALU.mult,
+                    )
+                    continue
                 for hl in range(HG):
                     h = hg * HG + hl
                     nc.scalar.activation(out=ctx_bfs[j][:, h, :], in_=c_ps[:, hl, :], func=ACT.Copy, scale=rinv[:, h, j : j + 1])
@@ -481,11 +514,14 @@ def tile_sparseattention_pa_kernel(tc, qh, kh, vh, Wo, bo, out):
                 c_gs[j][:].rearrange("p g q t -> p (g q t)"),
             )
 
-        def project(j):
+        def project(j, last):
             c_c, c_s = c_cs[j]
             for nh in range(2):
                 cols = slice(nh * N_HALF, (nh + 1) * N_HALF)
-                o_banks[j, nh] = psum_o.tile([P, N_HALF], F32, tag="o_ps", name="o_ps")
+                if last:
+                    o_banks[j, nh] = psum_f.tile([P, N_HALF], F32, tag="acc", name="o_ps")
+                else:
+                    o_banks[j, nh] = psum_o.tile([P, N_HALF], F32, tag="o_ps", name="o_ps")
                 for g in range(2):
                     mx_pass(
                         nc, o_banks[j, nh][:], c_c[:, g, :], c_s[:, g, :], w_c[:, g, cols], w_s[:, g, cols], g == 0, g == 1
@@ -502,11 +538,15 @@ def tile_sparseattention_pa_kernel(tc, qh, kh, vh, Wo, bo, out):
             nc.sync.dma_start(out=out_rows[:, j, cols], in_=o_sbs[j][:, cols])
 
         def r_turn(hg):
+            bank = psum_t.tile([P, 2, 2, P], F32, tag="tp")
             for g in range(2):
-                bank = psum_t.tile([P, PACK, P], BF16, tag="tp")
-                for t in range(PACK):
-                    nc.tensor.transpose(bank[:, t, :], e_r[:, hg, g * PACK + t, :], ident[:])
-                nc.scalar.copy(out=er_g[:, hg, g], in_=bank[:].rearrange("p t r -> p r t"))
+                words = e_r[:, hg, g].rearrange("r p t -> r (p t)").bitcast(F32)
+                for u in range(2):
+                    nc.tensor.transpose(bank[:, g, u, :], words[:, u : 2 * P : 2], ident32[:])
+            nc.scalar.copy(
+                out=er_g[:, hg].rearrange("p g r t -> p (g r t)").bitcast(F32).rearrange("p (g r u) -> p g r u", g=2, u=2),
+                in_=bank[:].rearrange("p g u r -> p g r u"),
+            )
 
         def r_quantise(hg):
             quantise(
@@ -519,18 +559,19 @@ def tile_sparseattention_pa_kernel(tc, qh, kh, vh, Wo, bo, out):
         def r_attend(hg):
             rc_ps = psum_f.tile([P, HG, DK], F32, tag="acc")
             rc_banks[hg] = rc_ps
-            heads = slice(hg * HG, (hg + 1) * HG)
-            for g in range(2):
-                mx_pass(
-                    nc,
-                    rc_ps[:].rearrange("r h d -> r (h d)"),
-                    er_c[:, hg, g, :],
-                    er_s[:, hg, g, :],
-                    v_c[:, g, heads, :].rearrange("p h d -> p (h d)"),
-                    v_s[:, g, heads, :].rearrange("p h d -> p (h d)"),
-                    start=(g == 0),
-                    stop=(g == 1),
-                )
+            for hl in range(HG):
+                h = hg * HG + hl
+                for g in range(2):
+                    mx_pass(
+                        nc,
+                        rc_ps[:, hl, :],
+                        er_c[:, hg, g, :],
+                        er_s[:, hg, g, :],
+                        v_c[:, h, g, :],
+                        v_s[:, h, g, :],
+                        start=(g == 0),
+                        stop=(g == 1),
+                    )
 
         def r_factors(hg):
             picks[hg] = stage.tile([P, HG], F32, tag="pick", name="pick")
@@ -559,16 +600,18 @@ def tile_sparseattention_pa_kernel(tc, qh, kh, vh, Wo, bo, out):
             ctx_r_ws[hg] = keep.tile([P, P], F32, name="ctx_r_w%d" % hg)
             nc.scalar.copy(out=ctx_r_ws[hg][:], in_=bank[:])
 
-        def weave(chain, fillers):
-            n = len(chain) + 1
+        def weave(chain, fillers, lead):
+            for f in fillers[:lead]:
+                f()
+            rest, n = fillers[lead:], max(1, len(chain))
             for i in range(n):
-                for f in fillers[i * len(fillers) // n : (i + 1) * len(fillers) // n]:
-                    f()
                 if i < len(chain):
                     chain[i]()
+                for f in rest[i * len(rest) // n : (i + 1) * len(rest) // n]:
+                    f()
 
         load_kq(0)
-        nc.vector.memset(va_raw[64:P].rearrange("p t d -> p (t d)").bitcast(I32), 0)
+        nc.gpsimd.memset(va_raw[64:P].rearrange("p t d -> p (t d)").bitcast(I32), 0)
         nc.sync.dma_start(
             out=va_raw[0:64],
             in_=vh[0].rearrange("h (x t s) d -> (h x) t s d", x=8, t=PACK)[:, :, 0, :],
@@ -605,12 +648,16 @@ def tile_sparseattention_pa_kernel(tc, qh, kh, vh, Wo, bo, out):
                 r_turn(0)
             if 1 <= s <= H:
                 v_regroup(s - 1)
+            if s == H + 0:
+                w_regroup_on_scalar(*w_units[3])
             if s == HG + 5:
                 r_attend(0)
 
             fillers, behind = behind, []
             if s == 1:
-                fillers += [va_regroup]
+                fillers += [make_mask_r] + [make_diag] + [open_mask_r]
+                fillers += [make_ident32, make_head_of, va_regroup, make_own_head]
+            if s == 2:
                 fillers += [lambda: nc.vector.memset(e_pad[:, :, H * NB : PACK * P].bitcast(I32), 0)]
                 fillers += va_spread()
                 behind += [va_quantise]
@@ -634,13 +681,12 @@ def tile_sparseattention_pa_kernel(tc, qh, kh, vh, Wo, bo, out):
                 chain += [lambda: find_highs(s - 1), lambda: find_top(s - 1), lambda: find_shifts(s - 1)]
             for hg in r_done:
                 chain += [lambda: r_highs(hg), lambda: r_top(hg), lambda: r_shift(hg)]
-            weave(chain, fillers)
+            weave(chain, fillers, len(fillers) // 4)
 
         order = [1, 2, 3, 4, 5, 0, 6, 7]
         fills = tile_fills(order[0])
         for j0 in range(0, NT, 2):
             turn_a(j0)
-        r_exps(1)
         for f in behind:
             f()
         nc.vector.tensor_tensor(out=rsum[:], in0=rsum_a[:], in1=e_own[:], op=ALU.add)
@@ -651,47 +697,51 @@ def tile_sparseattention_pa_kernel(tc, qh, kh, vh, Wo, bo, out):
         tile_quantise(order[0])
         for j0 in range(2, NT, 2):
             quantise_a(j0)
-        r_sum(1)
-        w_regroup(*w_units[3])
-        r_inverse(1)
-        for i in range(NT + 3):
+        w_quantise(*w_units[3])
+        for i in range(NT + 2):
             if i < NT:
-                attend(order[i])
+                attend(order[i], i == NT - 1)
+            if 1 <= i <= NT:
+                turn_ctx(order[i - 1])
             if i == 3:
                 r_turn_ctx(0)
             if i == 5:
                 r_turn_ctx(1)
-            if 1 <= i <= NT:
-                turn_ctx(order[i - 1])
-            if 2 <= i <= NT + 1:
-                project(order[i - 2])
+            if i >= 2:
+                project(order[i - 2], i == NT + 1)
             if i == 0:
+                r_exps(1)
+            if i == 1:
                 r_turn(1)
-            if i == 2:
+            if i == 3:
                 r_attend(1)
             if i + 1 < NT:
                 for f in tile_fills(order[i + 1]):
                     f()
-            if i == 0:
-                w_quantise(*w_units[3])
             if i == 1:
-                r_quantise(1)
-                r_factors(1)
+                r_sum(1)
             if i == 2:
+                r_inverse(1)
+                r_quantise(1)
                 r_pick(0)
             if i == 3:
+                r_factors(1)
+            if i == 4:
                 r_pick(1)
-            if i >= 3:
+            if 3 <= i <= NT:
                 add_bias(order[i - 3], 1)
                 store(order[i - 3], 1)
             if i + 1 < NT:
                 tile_quantise(order[i + 1])
             if i == 2:
                 r_join(0)
-            if i == 3:
+            if i == 4:
                 r_join(1)
             if 1 <= i <= NT:
                 quantise_ctx(order[i - 1])
-            if 2 <= i <= NT + 1:
+            if i >= 2:
                 add_bias(order[i - 2], 0)
                 store(order[i - 2], 0)
+            if i >= NT:
+                add_bias(order[i - 2], 1)
+                store(order[i - 2], 1)

@@ -268,8 +268,8 @@ def tile_sparseattention_pa_kernel(tc, qh, kh, vh, Wo, bo, out):
             nc.vector.tensor_tensor(out=top[:, h], in0=highs[:, h, :, 0], in1=highs[:, h, :, 1], op=ALU.max)
 
         def find_shifts(h):
-            nc.gpsimd.tensor_tensor(out=own_s[:, h], in0=highs[:, h, :, 1], in1=top[:, h], op=ALU.subtract)
-            nc.gpsimd.tensor_scalar(out=shift[:, h], in0=top[:, h], scalar1=-SCALE, scalar2=0.0, op0=ALU.mult, op1=ALU.add)
+            nc.vector.tensor_scalar(out=shift[:, h], in0=top[:, h], scalar1=-SCALE, scalar2=None, op0=ALU.mult)
+            nc.vector.tensor_tensor(out=own_s[:, h], in0=highs[:, h, :, 1], in1=top[:, h], op=ALU.subtract)
 
         def exps(h):
             nc.scalar.activation(out=e_own[:, h], in_=own_s[:, h], func=ACT.Exp, scale=SCALE)
@@ -611,7 +611,7 @@ def tile_sparseattention_pa_kernel(tc, qh, kh, vh, Wo, bo, out):
                     f()
 
         load_kq(0)
-        nc.gpsimd.memset(va_raw[64:P].rearrange("p t d -> p (t d)").bitcast(I32), 0)
+        nc.vector.memset(va_raw[64:P].rearrange("p t d -> p (t d)").bitcast(I32), 0)
         nc.sync.dma_start(
             out=va_raw[0:64],
             in_=vh[0].rearrange("h (x t s) d -> (h x) t s d", x=8, t=PACK)[:, :, 0, :],

@@ -28,6 +28,7 @@ SCALE = 1.0 / math.sqrt(DK)
 NQ = 4
 K_STEP = 160
 N_EARLY = 4
+W_STEPS = (1, 7, 8)
 N_KPAD = 3
 NEG = -1.0e30
 
@@ -205,12 +206,14 @@ def tile_sparseattention_pa_kernel(tc, qh, kh, vh, Wo, bo, out):
             v_raws[h] = loads.tile([P, 2, PACK, DK], BF16, tag="v_raw", name="v_raw")
             nc.sync.dma_start(out=v_raws[h][:], in_=vh[0, h].rearrange("(p g t) d -> p g t d", g=2, t=PACK))
 
-        def load_w(g):
-            w_raws[g] = loads.tile([P, PACK, D], BF16, tag="w_raw", bufs=2, name="w_raw")
-            nc.sync.dma_start(
-                out=w_raws[g][:].rearrange("p (u e) n -> p u e n", u=2),
-                in_=Wo.rearrange("(g u p e) n -> g p u e n", g=2, u=2, e=2)[g],
-            )
+        def load_w(g, nh):
+            w_raws[g, nh] = loads.tile([P, PACK, N_HALF], BF16, tag="w_raw", bufs=4, name="w_raw")
+            cols = slice(nh * N_HALF, (nh + 1) * N_HALF)
+            for u in range(2):
+                nc.sync.dma_start(
+                    out=w_raws[g, nh][:, 2 * u : 2 * u + 2, :],
+                    in_=Wo.rearrange("(g u p e) n -> g u p e n", g=2, u=2, e=2)[g, u][:, :, cols],
+                )
 
         def turn_keys(h):
             k_pad = k_pads[h % N_KPAD]
@@ -412,18 +415,17 @@ def tile_sparseattention_pa_kernel(tc, qh, kh, vh, Wo, bo, out):
             )
 
         def w_regroup(g, nh):
-            cols = slice(nh * N_HALF, (nh + 1) * N_HALF)
             w_gs[g, nh] = stage.tile([P, N_HALF, PACK], BF16, tag="w_g", align_bytes=64, name="w_g")
             nc.vector.tensor_copy(
                 out=w_gs[g, nh][:].rearrange("p (c i) t -> p c t i", i=4),
-                in_=w_raws[g][:, :, cols].rearrange("p t (c i) -> p c t i", i=4),
+                in_=w_raws[g, nh][:].rearrange("p t (c i) -> p c t i", i=4),
             )
 
         def w_regroup_on_scalar(g, nh):
             w_gs[g, nh] = stage.tile([P, N_HALF, PACK], BF16, tag="w_g", align_bytes=64, name="w_g")
             nc.scalar.copy(
                 out=w_gs[g, nh][:].rearrange("p (c i) t -> p c t i", i=4),
-                in_=w_raws[g][:, :, nh * N_HALF : (nh + 1) * N_HALF].rearrange("p t (c i) -> p c t i", i=4),
+                in_=w_raws[g, nh][:].rearrange("p t (c i) -> p c t i", i=4),
             )
 
         def w_quantise(g, nh):
@@ -529,7 +531,7 @@ def tile_sparseattention_pa_kernel(tc, qh, kh, vh, Wo, bo, out):
 
         def add_bias(j, nh):
             if nh == 0:
-                o_sbs[j] = stage.tile([P, D], F32, tag="o_sb", bufs=3, name="o_sb")
+                o_sbs[j] = loads.tile([P, D], F32, tag="w_raw", bufs=4, name="o_sb")
             cols = slice(nh * N_HALF, (nh + 1) * N_HALF)
             nc.vector.tensor_tensor(out=o_sbs[j][:, cols], in0=o_banks[j, nh][:], in1=bias[:, cols], op=ALU.add)
 
@@ -610,7 +612,9 @@ def tile_sparseattention_pa_kernel(tc, qh, kh, vh, Wo, bo, out):
                 for f in rest[i * len(rest) // n : (i + 1) * len(rest) // n]:
                     f()
 
+        w_units = [(g, nh) for g in range(2) for nh in range(2)]
         load_kq(0)
+        load_w(*w_units[0])
         nc.vector.memset(va_raw[64:P].rearrange("p t d -> p (t d)").bitcast(I32), 0)
         nc.sync.dma_start(
             out=va_raw[0:64],
@@ -618,26 +622,27 @@ def tile_sparseattention_pa_kernel(tc, qh, kh, vh, Wo, bo, out):
         )
         load_kq(1)
         load_v(0)
-        w_units = [(g, nh) for g in range(2) for nh in range(2)]
         behind = []
         for s in range(H + 2):
             if s + 2 < H:
                 load_kq(s + 2)
             if s + 1 < H:
                 load_v(s + 1)
-            if s in (2, 3):
-                load_w(s - 2)
+            if 1 <= s < 4:
+                load_w(*w_units[s])
             if s == 4:
                 nc.sync.dma_start(out=bias[:], in_=bo.partition_broadcast(P))
             r_done = [hg for hg in range(2) if s == HG * hg + HG + 1]
             r_ready = [hg for hg in range(2) if s == HG * hg + HG + 2]
 
-            if s < H:
+            if s < H and s != 1:
                 turn_keys(s)
             for hg in r_ready:
                 r_exps(hg)
             if 1 <= s <= H:
                 scores(s - 1)
+            if s == 1:
+                turn_keys(s)
             if s >= 2:
                 exps(s - 2)
             if s < H:
@@ -656,18 +661,17 @@ def tile_sparseattention_pa_kernel(tc, qh, kh, vh, Wo, bo, out):
             fillers, behind = behind, []
             if s == 1:
                 fillers += [make_mask_r] + [make_diag] + [open_mask_r]
-                fillers += [make_ident32, make_head_of, va_regroup, make_own_head]
+                fillers += [make_ident32, make_head_of, va_regroup, make_own_head] + va_spread()
+                behind += [va_quantise]
             if s == 2:
                 fillers += [lambda: nc.vector.memset(e_pad[:, :, H * NB : PACK * P].bitcast(I32), 0)]
-                fillers += va_spread()
-                behind += [va_quantise]
             if s >= 2:
                 fillers = [lambda h=s - 2: v_quantise(h)] + fillers
             if 3 <= s < N_EARLY + 3:
                 fillers += head_fills(s - 3)
                 behind += [lambda h=s - 3: head_quantise(h)]
-            if N_EARLY + 2 <= s < N_EARLY + 5:
-                unit = w_units[s - N_EARLY - 2]
+            if s in W_STEPS:
+                unit = w_units[W_STEPS.index(s)]
                 fillers += [lambda u=unit: w_regroup(*u)]
                 behind += [lambda u=unit: w_quantise(*u)]
             if s == HG + 3:
@@ -677,11 +681,11 @@ def tile_sparseattention_pa_kernel(tc, qh, kh, vh, Wo, bo, out):
             if s == HG + 5:
                 fillers += [lambda: r_factors(0)]
             chain = []
-            if 1 <= s <= H:
-                chain += [lambda: find_highs(s - 1), lambda: find_top(s - 1), lambda: find_shifts(s - 1)]
             for hg in r_done:
                 chain += [lambda: r_highs(hg), lambda: r_top(hg), lambda: r_shift(hg)]
-            weave(chain, fillers, len(fillers) // 4)
+            if 1 <= s <= H:
+                chain += [lambda: find_highs(s - 1), lambda: find_top(s - 1), lambda: find_shifts(s - 1)]
+            weave(chain, fillers, len(fillers) if s == 1 else len(fillers) // 4)
 
         order = [1, 2, 3, 4, 5, 0, 6, 7]
         fills = tile_fills(order[0])

@@ -69,17 +69,16 @@ def tile_sparseattention_pa_kernel(tc, qh, kh, vh, Wo, bo, out):
 
         k_pads = [keep.tile([P, NT, NQ * K_STEP], BF16, name="k_pad%d" % i) for i in range(N_KPAD)]
 
-        runs = [
-            k_pad[:].rearrange("d j c -> d (j c)").bitcast(F32).rearrange("d (r c) -> d r c", c=K_STEP // 2)[:, :, NB // 2 :]
-            for k_pad in k_pads
-        ]
         n_gap = (K_STEP - NB) // 2
+        gaps = [
+            k_pad[:].bitcast(F32).rearrange("d j (q c) -> d j q c", q=NQ)[:, :, 0 : NQ - 1, NB // 2 :] for k_pad in k_pads
+        ]
         zero = const.tile([P, n_gap], F32)
         nc.vector.memset(zero[:], 0.0)
         one = const.tile([P, 1], F32)
         nc.scalar.activation(out=one[:], in_=zero[:, 0:1], func=ACT.Exp)
-        nc.vector.memset(runs[0].bitcast(I32), 0)
-        nc.scalar.copy(out=runs[1], in_=zero[:].unsqueeze(1).to_broadcast([P, NT * NQ, n_gap]))
+        nc.vector.memset(gaps[0].bitcast(I32), 0)
+        nc.scalar.copy(out=gaps[2], in_=zero[:].unsqueeze(1).unsqueeze(1).to_broadcast([P, NT, NQ - 1, n_gap]))
         qs_pad = keep.tile([P, H, P], BF16)
         nc.vector.memset(qs_pad[:].bitcast(I32), 0)
 
@@ -122,7 +121,7 @@ def tile_sparseattention_pa_kernel(tc, qh, kh, vh, Wo, bo, out):
             base=NB - 1,
             channel_multiplier=-8,
         )
-        nc.gpsimd.memset(runs[2].bitcast(I32), 0)
+        nc.vector.memset(gaps[1].bitcast(I32), 0)
         mask_r = const.tile([P, NT, P], BF16)
         ident32 = const.tile([P, P], F32)
         head_of = const.tile([P, H], F32)

from contextlib import ExitStack
import math

import concourse.mybir as mybir
from concourse.masks import make_identity

BF16 = mybir.dt.bfloat16
F32 = mybir.dt.float32
U32 = mybir.dt.uint32
U8 = mybir.dt.uint8
I32 = mybir.dt.int32
FP8X4 = mybir.dt.float8_e4m3fn_x4
ALU = mybir.AluOpType
ACT = mybir.ActivationFunctionType
AXIS_X = mybir.AxisListType.X

P = 128
H = 8
S = 1024
DK = 128
D = H * DK
NT = S // P
NB = 32
PACK = 4
HG = 4
N_HALF = 512
SCALE = 1.0 / math.sqrt(DK)
NQ = 4
K_STEP = 160
N_EARLY = 4
W_STEPS = (1, 7, 8)
N_KPAD = 3
NEG = -1.0e30

FLOPS = 3 * 2 * S * S * D


def quantise(nc, codes, scales, grouped):
    nc.vector.quantize_mx(out=codes.bitcast(FP8X4), scales=scales, in_=grouped)


def mx_pass(nc, acc, lhs, lhs_scale, rhs, rhs_scale, start, stop):
    nc.tensor.matmul_mx(
        out=acc,
        lhsT=lhs.bitcast(FP8X4),
        lhsT_scale=lhs_scale,
        rhs=rhs.bitcast(FP8X4),
        rhs_scale=rhs_scale,
        start=start,
        stop=stop,
    )


def tile_sparseattention_pa_kernel(tc, qh, kh, vh, Wo, bo, out):
    nc = tc.nc
    with ExitStack() as ctx:
        const = ctx.enter_context(tc.tile_pool(name="const", bufs=1))
        keep = ctx.enter_context(tc.tile_pool(name="keep", bufs=1))
        loads = ctx.enter_context(tc.tile_pool(name="loads", bufs=3))
        stage = ctx.enter_context(tc.tile_pool(name="stage", bufs=2))
        psum_t = ctx.enter_context(tc.psum_pool(name="psum_t", bufs=3))
        psum_f = ctx.enter_context(tc.psum_pool(name="psum_f", bufs=3))
        psum_o = ctx.enter_context(tc.psum_pool(name="psum_o", bufs=2))

        ctx.enter_context(tc.manual_schedule())

        ident = const.tile([P, P], BF16)
        make_identity(nc, ident[:])

        k_pads = [keep.tile([P, NT, NQ * K_STEP], BF16, name="k_pad%d" % i) for i in range(N_KPAD)]

        n_gap = (K_STEP - NB) // 2
        gaps = [
            k_pad[:].bitcast(F32).rearrange("d j (q c) -> d j q c", q=NQ)[:, :, 0 : NQ - 1, NB // 2 :] for k_pad in k_pads
        ]
        zero = const.tile([P, n_gap], F32)
        nc.vector.memset(zero[:], 0.0)
        one = const.tile([P, 1], F32)
        nc.scalar.activation(out=one[:], in_=zero[:, 0:1], func=ACT.Exp)
        nc.vector.memset(gaps[0].bitcast(I32), 0)
        nc.scalar.copy(out=gaps[2], in_=zero[:].unsqueeze(1).unsqueeze(1).to_broadcast([P, NT, NQ - 1, n_gap]))
        qs_pad = keep.tile([P, H, P], BF16)
        nc.vector.memset(qs_pad[:].bitcast(I32), 0)

        n_diag = PACK * P
        diag = const.tile([P, PACK * (n_diag + 1)], BF16)
        nc.vector.memset(diag[:].bitcast(I32), 0)
        mask_a32 = const.tile([P, NT, NB], F32)
        nc.gpsimd.memset(mask_a32[:], 0.0)
        nc.gpsimd.affine_select(
            out=mask_a32[:],
            in_=mask_a32[:],
            pattern=[[1, NT], [-NB, NB]],
            compare_op=ALU.is_ge,
            fill=NEG,
            base=0,
            channel_multiplier=NT,
        )
        mask_s = const.tile([P, NT, 2, NB], BF16)
        nc.vector.tensor_copy(out=mask_s[:, :, 0, :], in_=mask_a32[:])
        own32 = const.tile([P, NB], F32)
        nc.vector.tensor_reduce(
            out=own32[:], in_=ident[:].rearrange("p (q c) -> p c q", q=NQ), axis=AXIS_X, op=ALU.add
        )
        nc.vector.tensor_scalar(
            out=mask_s[:, :, 1, :],
            in0=own32[:].unsqueeze(1).to_broadcast([P, NT, NB]),
            scalar1=-1.0,
            scalar2=-NEG,
            op0=ALU.add,
            op1=ALU.mult,
        )
        mask_r32 = const.tile([P, NB, PACK], F32)
        nc.gpsimd.memset(mask_r32[:], 0.0)
        nc.gpsimd.affine_select(
            out=mask_r32[:],
            in_=mask_r32[:],
            pattern=[[NB, NB], [0, PACK]],
            compare_op=ALU.is_ge,
            fill=NEG,
            base=NB - 1,
            channel_multiplier=-8,
        )
        nc.vector.memset(gaps[1].bitcast(I32), 0)
        mask_r = const.tile([P, NT, P], BF16)
        ident32 = const.tile([P, P], F32)
        head_of = const.tile([P, H], F32)
        own_head = const.tile([P, HG], F32)

        def make_mask_r():
            nc.vector.tensor_copy(
                out=mask_r[:], in_=mask_r32[:].rearrange("r a b -> r (a b)").unsqueeze(1).to_broadcast([P, NT, P])
            )

        def open_mask_r():
            nc.vector.memset(mask_r[:, 0, 0:P:PACK], 0.0)

        def make_ident32():
            nc.vector.tensor_copy(out=ident32[:], in_=ident[:])

        def make_diag():
            nc.vector.tensor_copy(
                out=diag[:].rearrange("p (t x) -> p t x", t=PACK)[:, :, 0:n_diag:PACK],
                in_=ident[:].unsqueeze(1).to_broadcast([P, PACK, P]),
            )

        def make_head_of():
            nc.vector.tensor_reduce(
                out=head_of[:],
                in_=ident[:, 0 : H * 8].rearrange("p (h x) -> p h x", x=8),
                axis=AXIS_X,
                op=ALU.add,
            )

        def make_own_head():
            nc.vector.tensor_reduce(
                out=own_head[:],
                in_=ident[:].rearrange("p (a h) -> p h a", h=HG),
                axis=AXIS_X,
                op=ALU.add,
            )

        highs = keep.tile([P, H, NT, 2], F32)
        top = keep.tile([P, H, NT], F32)
        shift = keep.tile([P, H, NT], F32)
        own_s = keep.tile([P, H, NT], F32)
        e_own = keep.tile([P, H, NT], F32)
        rsum_a = keep.tile([P, H, NT], F32)
        rsum = keep.tile([P, H, NT], F32)
        rinv = keep.tile([P, H, NT], F32)
        e_pad = keep.tile([P, NT, PACK * P], BF16)
        ea_c = keep.tile([P, NT, P], U32, align_bytes=64)
        ea_s = keep.tile([P, NT, P], U8, align_bytes=64)
        eb_c = keep.tile([P, N_EARLY, NT, P], U32, align_bytes=64)
        eb_s = keep.tile([P, N_EARLY, NT, P], U8, align_bytes=64)
        ebl_c = keep.tile([P, NT, H - N_EARLY, P], U32, align_bytes=64)
        ebl_s = keep.tile([P, NT, H - N_EARLY, P], U8, align_bytes=64)
        v_c = keep.tile([P, H, 2, DK], U32, align_bytes=64)
        v_s = keep.tile([P, H, 2, DK], U8, align_bytes=64)
        va_raw = keep.tile([P, PACK, DK], BF16)
        va_w = keep.tile([P, DK, PACK], BF16)
        va_c = keep.tile([P, H, DK], U32, align_bytes=64)
        va_s = keep.tile([P, H, DK], U8, align_bytes=64)
        w_c = keep.tile([P, 2, D], U32, align_bytes=64)
        w_s = keep.tile([P, 2, D], U8, align_bytes=64)
        bias = keep.tile([P, D], BF16)
        e_r = keep.tile([P, 2, 2, P, PACK], BF16)
        top_r = keep.tile([P, 2, 2], F32)
        shift_r = keep.tile([P, 2], F32)
        rsum_r = keep.tile([P, 2, 2], F32)
        rinv_r = keep.tile([P, 2], F32)
        er_g = keep.tile([P, 2, 2, P, PACK], BF16, align_bytes=64)
        er_c = keep.tile([P, 2, 2, P], U32, align_bytes=64)
        er_s = keep.tile([P, 2, 2, P], U8, align_bytes=64)

        nats, q_ts, s_banks, r_banks, v_raws, v_gs, w_raws, w_gs, eb_gs = {}, {}, {}, {}, {}, {}, {}, {}, {}

        def load_kq(h):
            for name, src in (("k_nat", kh), ("q_nat", qh)):
                nat = loads.tile([P, NT, DK], BF16, tag=name, name=name)
                nc.sync.dma_start(out=nat[:], in_=src[0, h].rearrange("(p j) d -> p j d", j=NT))
                nats[name, h] = nat

        def load_v(h):
            v_raws[h] = loads.tile([P, 2, PACK, DK], BF16, tag="v_raw", name="v_raw")
            nc.sync.dma_start(out=v_raws[h][:], in_=vh[0, h].rearrange("(p g t) d -> p g t d", g=2, t=PACK))

        def load_w(g, nh):
            w_raws[g, nh] = loads.tile([P, PACK, N_HALF], BF16, tag="w_raw", bufs=4, name="w_raw")
            cols = slice(nh * N_HALF, (nh + 1) * N_HALF)
            for u in range(2):
                nc.sync.dma_start(
                    out=w_raws[g, nh][:, 2 * u : 2 * u + 2, :],
                    in_=Wo.rearrange("(g u p e) n -> g u p e n", g=2, u=2, e=2)[g, u][:, :, cols],
                )

        def turn_keys(h):
            k_pad = k_pads[h % N_KPAD]
            for j0 in range(0, NT, PACK):
                bank = psum_t.tile([P, PACK, P], BF16, tag="tp")
                for j in range(j0, j0 + PACK):
                    nc.tensor.transpose(bank[:, j - j0, :], nats["k_nat", h][:, j, :], ident[:])
                nc.scalar.copy(
                    out=k_pad[:, j0 : j0 + PACK].rearrange("d j (q c) -> d j q c", q=NQ)[:, :, :, 0:NB],
                    in_=bank[:].rearrange("d j (q c) -> d j q c", q=NQ),
                )

        def turn_queries(h):
            q_t = loads.tile([P, NT, P], BF16, tag="q_t")
            q_ts[h] = q_t
            for j0 in range(0, NT, PACK):
                bank = psum_t.tile([P, PACK, P], BF16, tag="tp")
                for j in range(j0, j0 + PACK):
                    nc.tensor.transpose(bank[:, j - j0, :], nats["q_nat", h][:, j, :], ident[:])
                nc.scalar.copy(out=q_t[:, j0 : j0 + PACK], in_=bank[:])
            nc.scalar.copy(out=qs_pad[:, h, h % HG : P : HG], in_=q_t[:, 0, 0:P:PACK])

        def scores(h):
            q_t, k_pad = q_ts[h], k_pads[h % N_KPAD]
            s_ps = psum_f.tile([P, NT, 2, NB], F32, tag="acc")
            s_banks[h] = s_ps
            nc.tensor.matmul(
                out=s_ps[:].rearrange("p j i c -> p (j i c)"),
                lhsT=ident[:],
                rhs=mask_s[:].rearrange("p j i c -> p (j i c)"),
                start=True,
                stop=False,
            )
            for j in range(NT):
                nc.tensor.matmul(
                    out=s_ps[:, j, 0, :],
                    lhsT=q_t[:, j, :],
                    rhs=k_pad[:, 0, :].rearrange("d (q c) -> d q c", q=NQ)[:, :, 0:NB:PACK],
                    start=False,
                    stop=False,
                )
                for q in range(NQ):
                    nc.tensor.matmul(
                        out=s_ps[:, j, 1, :],
                        lhsT=k_pad[:, j, q * P : (q + 1) * P],
                        rhs=q_t[:, j, q * NB : (q + 1) * NB],
                        start=False,
                        stop=(j == NT - 1 and q == NQ - 1),
                    )

        def find_highs(h):
            nc.vector.tensor_reduce(out=highs[:, h], in_=s_banks[h][:], axis=AXIS_X, op=ALU.max)

        def find_top(h):
            nc.vector.tensor_tensor(out=top[:, h], in0=highs[:, h, :, 0], in1=highs[:, h, :, 1], op=ALU.max)

        def find_shifts(h):
            nc.vector.tensor_scalar(out=shift[:, h], in0=top[:, h], scalar1=-SCALE, scalar2=None, op0=ALU.mult)
            nc.vector.tensor_tensor(out=own_s[:, h], in0=highs[:, h, :, 1], in1=top[:, h], op=ALU.subtract)

        def exps(h):
            nc.scalar.activation(out=e_own[:, h], in_=own_s[:, h], func=ACT.Exp, scale=SCALE)
            for j in range(NT):
                nc.scalar.activation(
                    out=e_pad[:, j, h * NB : (h + 1) * NB],
                    in_=s_banks[h][:, j, 0, :],
                    func=ACT.Exp,
                    bias=shift[:, h, j : j + 1],
                    scale=SCALE,
                    accum_out=rsum_a[:, h, j : j + 1],
                )

        def r_scores(h):
            hg, hl = divmod(h, HG)
            k_pad = k_pads[h % N_KPAD]
            for half in range(2):
                if hl == 0:
                    r_banks[hg, half] = psum_o.tile([P, N_HALF], F32, tag="o_ps", name="r_ps%d" % half)
                    nc.tensor.matmul(
                        out=r_banks[hg, half][:],
                        lhsT=ident[:],
                        rhs=mask_r[:, half * PACK : (half + 1) * PACK, :].rearrange("r j p -> r (j p)"),
                        start=True,
                        stop=False,
                    )
                nc.tensor.matmul(
                    out=r_banks[hg, half][:].rearrange("r (j q c) -> r j q c", j=PACK, q=NQ),
                    lhsT=qs_pad[:, h, :],
                    rhs=k_pad[:, half * PACK : (half + 1) * PACK].rearrange("d j (q c) -> d j q c", q=NQ)[:, :, :, 0:NB],
                    start=False,
                    stop=(hl == HG - 1),
                )

        def r_highs(hg):
            for half in range(2):
                nc.vector.tensor_reduce(
                    out=top_r[:, hg, half : half + 1], in_=r_banks[hg, half][:], axis=AXIS_X, op=ALU.max
                )

        def r_top(hg):
            nc.vector.tensor_tensor(
                out=shift_r[:, hg : hg + 1], in0=top_r[:, hg, 0:1], in1=top_r[:, hg, 1:2], op=ALU.max
            )

        def r_shift(hg):
            nc.vector.tensor_scalar(
                out=shift_r[:, hg : hg + 1], in0=shift_r[:, hg : hg + 1], scalar1=-SCALE, scalar2=None, op0=ALU.mult
            )

        def r_exps(hg):
            for half in range(2):
                nc.scalar.activation(
                    out=e_r[:, hg, half],
                    in_=r_banks[hg, half][:].rearrange("r (t p) -> r p t", t=PACK),
                    func=ACT.Exp,
                    bias=shift_r[:, hg : hg + 1],
                    scale=SCALE,
                    accum_out=rsum_r[:, hg, half : half + 1],
                )

        def r_sum(hg):
            nc.vector.tensor_tensor(
                out=rinv_r[:, hg : hg + 1], in0=rsum_r[:, hg, 0:1], in1=rsum_r[:, hg, 1:2], op=ALU.add
            )

        def r_inverse(hg):
            nc.vector.reciprocal(out=rinv_r[:, hg : hg + 1], in_=rinv_r[:, hg : hg + 1])

        def fill(eb_g, slot, h, j):
            nc.vector.tensor_scalar(
                out=eb_g[:, slot].rearrange("p c t -> p (c t)"),
                in0=diag[:, j % PACK * n_diag : (j % PACK + 1) * n_diag],
                scalar1=e_own[:, h, j : j + 1],
                scalar2=None,
                op0=ALU.mult,
            )

        def head_fills(h):
            eb_gs["head", h] = stage.tile([P, NT, P, PACK], BF16, tag="eb_g", align_bytes=64, name="eb_g")
            return [lambda j=j: fill(eb_gs["head", h], j, h, j) for j in range(NT)]

        def head_quantise(h):
            quantise(
                nc,
                eb_c[:, h].rearrange("p j c -> p (j c)"),
                eb_s[:, h].rearrange("p j c -> p (j c)"),
                eb_gs["head", h][:].rearrange("p j c t -> p (j c t)"),
            )

        def tile_fills(j):
            eb_gs["tile", j] = stage.tile([P, H - N_EARLY, P, PACK], BF16, tag="eb_g", align_bytes=64, name="eb_g")
            return [lambda h=h: fill(eb_gs["tile", j], h - N_EARLY, h, j) for h in range(N_EARLY, H)]

        def tile_quantise(j):
            quantise(
                nc,
                ebl_c[:, j].rearrange("p h c -> p (h c)"),
                ebl_s[:, j].rearrange("p h c -> p (h c)"),
                eb_gs["tile", j][:].rearrange("p h c t -> p (h c t)"),
            )

        def v_regroup(h):
            v_gs[h] = stage.tile([P, 2, DK, PACK], BF16, tag="v_g", align_bytes=64, name="v_g")
            for g in range(2):
                nc.scalar.copy(
                    out=v_gs[h][:, g].rearrange("p (c i) t -> p c t i", i=4),
                    in_=v_raws[h][:, g].rearrange("p t (c i) -> p c t i", i=4),
                )

        def v_quantise(h):
            quantise(
                nc,
                v_c[:, h].rearrange("p g d -> p (g d)"),
                v_s[:, h].rearrange("p g d -> p (g d)"),
                v_gs[h][:].rearrange("p g d t -> p (g d t)"),
            )

        va_gs = []

        def va_regroup():
            nc.vector.tensor_copy(out=va_w[:], in_=va_raw[:].rearrange("p t d -> p d t"))

        def va_spread():
            va_gs.append(stage.tile([P, H, DK, PACK], BF16, tag="eb_g", align_bytes=64, name="va_g"))

            def spread(h):
                nc.vector.tensor_scalar(
                    out=va_gs[0][:, h], in0=va_w[:], scalar1=head_of[:, h : h + 1], scalar2=None, op0=ALU.mult
                )

            return [lambda h=h: spread(h) for h in range(H)]

        def va_quantise():
            quantise(
                nc,
                va_c[:].rearrange("p h d -> p (h d)"),
                va_s[:].rearrange("p h d -> p (h d)"),
                va_gs[0][:].rearrange("p h d t -> p (h d t)"),
            )

        def w_regroup(g, nh):
            w_gs[g, nh] = stage.tile([P, N_HALF, PACK], BF16, tag="w_g", align_bytes=64, name="w_g")
            nc.vector.tensor_copy(
                out=w_gs[g, nh][:].rearrange("p (c i) t -> p c t i", i=4),
                in_=w_raws[g, nh][:].rearrange("p t (c i) -> p c t i", i=4),
            )

        def w_regroup_on_scalar(g, nh):
            w_gs[g, nh] = stage.tile([P, N_HALF, PACK], BF16, tag="w_g", align_bytes=64, name="w_g")
            nc.scalar.copy(
                out=w_gs[g, nh][:].rearrange("p (c i) t -> p c t i", i=4),
                in_=w_raws[g, nh][:].rearrange("p t (c i) -> p c t i", i=4),
            )

        def w_quantise(g, nh):
            cols = slice(nh * N_HALF, (nh + 1) * N_HALF)
            quantise(nc, w_c[:, g, cols], w_s[:, g, cols], w_gs[g, nh][:].rearrange("p n t -> p (n t)"))

        out_rows = out[0].rearrange("(p j) n -> p j n", j=NT)
        ea_gs, c_banks, ctx_bfs, c_gs, c_cs, o_banks, o_sbs = {}, {}, {}, {}, {}, {}, {}
        er_gs, ctx_rs, picks, pickeds, rc_banks, ctx_r_ws = {}, {}, {}, {}, {}, {}

        def turn_a(j0):
            ea_gs[j0] = stage.tile([P, 2, P, PACK], BF16, tag="ea_g", align_bytes=64, name="ea_g")
            bank = psum_t.tile([P, 2, 2, P], F32, tag="tp")
            for j in range(j0, j0 + 2):
                words = e_pad[:, j, :].bitcast(F32)
                for u in range(2):
                    nc.tensor.transpose(bank[:, j - j0, u, :], words[:, u : 2 * P : 2], ident32[:])
            nc.scalar.copy(
                out=ea_gs[j0][:].rearrange("p j q t -> p j (q t)").bitcast(F32).rearrange("p j (q u) -> p j q u", u=2),
                in_=bank[:].rearrange("p j u q -> p j q u"),
            )

        def quantise_a(j0):
            quantise(
                nc,
                ea_c[:, j0 : j0 + 2, :].rearrange("p j q -> p (j q)"),
                ea_s[:, j0 : j0 + 2, :].rearrange("p j q -> p (j q)"),
                ea_gs[j0][:].rearrange("p j q t -> p (j q t)"),
            )

        def attend(j, on_vector):
            ctx_bfs[j] = stage.tile([P, H, DK], BF16, tag="ctx_bf", name="ctx_bf")
            for hg in range(2):
                heads = slice(hg * HG, (hg + 1) * HG)
                c_ps = psum_f.tile([P, HG, DK], F32, tag="acc")
                mx_pass(
                    nc, c_ps[:].rearrange("p h d -> p (h d)"), ea_c[:, j, :], ea_s[:, j, :],
                    va_c[:, heads, :].rearrange("p h d -> p (h d)"), va_s[:, heads, :].rearrange("p h d -> p (h d)"), True, False,
                )
                for hl in range(HG):
                    h = hg * HG + hl
                    if h < N_EARLY:
                        e_codes, e_scales = eb_c[:, h, j, :], eb_s[:, h, j, :]
                    else:
                        e_codes, e_scales = ebl_c[:, j, h - N_EARLY, :], ebl_s[:, j, h - N_EARLY, :]
                    mx_pass(
                        nc, c_ps[:, hl, :], e_codes, e_scales,
                        v_c[:, h, j // PACK, :], v_s[:, h, j // PACK, :], False, hl == HG - 1,
                    )
                if hg == 1 and on_vector:
                    nc.vector.tensor_tensor(
                        out=ctx_bfs[j][:, heads],
                        in0=c_ps[:],
                        in1=rinv[:, heads, j].unsqueeze(2).to_broadcast([P, HG, DK]),
                        op=ALU.mult,
                    )
                    continue
                for hl in range(HG):
                    h = hg * HG + hl
                    nc.scalar.activation(out=ctx_bfs[j][:, h, :], in_=c_ps[:, hl, :], func=ACT.Copy, scale=rinv[:, h, j : j + 1])

        def turn_ctx(j):
            bank = psum_t.tile([P, 2, 2, P], F32, tag="tp")
            for hg in range(2):
                words = ctx_bfs[j][:, hg * HG : (hg + 1) * HG, :].rearrange("p h d -> p (h d)").bitcast(F32)
                for u in range(2):
                    nc.tensor.transpose(bank[:, hg, u, :], words[:, u * P : (u + 1) * P], ident32[:])
            c_gs[j] = stage.tile([P, 2, P, PACK], BF16, tag="c_g", align_bytes=64, name="c_g")
            c_gw = c_gs[j][:].rearrange("p g q t -> p (g q t)").bitcast(F32).rearrange("p (g q u) -> p g q u", g=2, u=2)
            nc.scalar.copy(out=c_gw, in_=bank[:].rearrange("p g u q -> p g q u"))
            if j == 0:
                for hg in range(2):
                    for f in range(2):
                        rows = slice(64 * f, 64 * (f + 1))
                        nc.scalar.copy(
                            out=c_gw[rows, hg, 0:P:PACK, :],
                            in_=ctx_r_ws[hg][rows].rearrange("d (a u f) -> d a u f", u=2, f=2)[:, :, :, f],
                        )

        def quantise_ctx(j):
            c_c = stage.tile([P, 2, P], U32, tag="c_c", align_bytes=64)
            c_s = stage.tile([P, 2, P], U8, tag="c_s", align_bytes=64)
            c_cs[j] = (c_c, c_s)
            quantise(
                nc,
                c_c[:].rearrange("p g q -> p (g q)"),
                c_s[:].rearrange("p g q -> p (g q)"),
                c_gs[j][:].rearrange("p g q t -> p (g q t)"),
            )

        def project(j, last):
            c_c, c_s = c_cs[j]
            for nh in range(2):
                cols = slice(nh * N_HALF, (nh + 1) * N_HALF)
                if last:
                    o_banks[j, nh] = psum_f.tile([P, N_HALF], F32, tag="acc", name="o_ps")
                else:
                    o_banks[j, nh] = psum_o.tile([P, N_HALF], F32, tag="o_ps", name="o_ps")
                for g in range(2):
                    mx_pass(
                        nc, o_banks[j, nh][:], c_c[:, g, :], c_s[:, g, :], w_c[:, g, cols], w_s[:, g, cols], g == 0, g == 1
                    )

        def add_bias(j, nh):
            if nh == 0:
                o_sbs[j] = loads.tile([P, D], F32, tag="w_raw", bufs=4, name="o_sb")
            cols = slice(nh * N_HALF, (nh + 1) * N_HALF)
            nc.vector.tensor_tensor(out=o_sbs[j][:, cols], in0=o_banks[j, nh][:], in1=bias[:, cols], op=ALU.add)

        def store(j, nh):
            cols = slice(nh * N_HALF, (nh + 1) * N_HALF)
            nc.sync.dma_start(out=out_rows[:, j, cols], in_=o_sbs[j][:, cols])

        def r_turn(hg):
            bank = psum_t.tile([P, 2, 2, P], F32, tag="tp")
            for g in range(2):
                words = e_r[:, hg, g].rearrange("r p t -> r (p t)").bitcast(F32)
                for u in range(2):
                    nc.tensor.transpose(bank[:, g, u, :], words[:, u : 2 * P : 2], ident32[:])
            nc.scalar.copy(
                out=er_g[:, hg].rearrange("p g r t -> p (g r t)").bitcast(F32).rearrange("p (g r u) -> p g r u", g=2, u=2),
                in_=bank[:].rearrange("p g u r -> p g r u"),
            )

        def r_quantise(hg):
            quantise(
                nc,
                er_c[:, hg].rearrange("p g r -> p (g r)"),
                er_s[:, hg].rearrange("p g r -> p (g r)"),
                er_g[:, hg].rearrange("p g r t -> p (g r t)"),
            )

        def r_attend(hg):
            rc_ps = psum_f.tile([P, HG, DK], F32, tag="acc")
            rc_banks[hg] = rc_ps
            for hl in range(HG):
                h = hg * HG + hl
                for g in range(2):
                    mx_pass(
                        nc,
                        rc_ps[:, hl, :],
                        er_c[:, hg, g, :],
                        er_s[:, hg, g, :],
                        v_c[:, h, g, :],
                        v_s[:, h, g, :],
                        start=(g == 0),
                        stop=(g == 1),
                    )

        def r_factors(hg):
            picks[hg] = stage.tile([P, HG], F32, tag="pick", name="pick")
            nc.vector.tensor_scalar(
                out=picks[hg][:], in0=own_head[:], scalar1=rinv_r[:, hg : hg + 1], scalar2=None, op0=ALU.mult
            )

        def r_pick(hg):
            pickeds[hg] = stage.tile([P, HG, DK], F32, tag="picked", name="picked")
            nc.vector.tensor_tensor(
                out=pickeds[hg][:],
                in0=rc_banks[hg][:],
                in1=picks[hg][:].unsqueeze(2).to_broadcast([P, HG, DK]),
                op=ALU.mult,
            )

        def r_join(hg):
            ctx_rs[hg] = stage.tile([P, 2, DK], BF16, tag="ctx_r", name="ctx_r")
            nc.vector.tensor_tensor(
                out=ctx_rs[hg][:], in0=pickeds[hg][:, 0:2, :], in1=pickeds[hg][:, 2:4, :], op=ALU.add
            )

        def r_turn_ctx(hg):
            bank = psum_t.tile([P, P], F32, tag="tp")
            nc.tensor.transpose(bank[:], ctx_rs[hg][:].rearrange("r f d -> r (f d)").bitcast(F32), ident32[:])
            ctx_r_ws[hg] = keep.tile([P, P], F32, name="ctx_r_w%d" % hg)
            nc.scalar.copy(out=ctx_r_ws[hg][:], in_=bank[:])

        def weave(chain, fillers, lead):
            for f in fillers[:lead]:
                f()
            rest, n = fillers[lead:], max(1, len(chain))
            for i in range(n):
                if i < len(chain):
                    chain[i]()
                for f in rest[i * len(rest) // n : (i + 1) * len(rest) // n]:
                    f()

        w_units = [(g, nh) for g in range(2) for nh in range(2)]
        load_kq(0)
        load_w(*w_units[0])
        nc.vector.memset(va_raw[64:P].rearrange("p t d -> p (t d)").bitcast(I32), 0)
        nc.sync.dma_start(
            out=va_raw[0:64],
            in_=vh[0].rearrange("h (x t s) d -> (h x) t s d", x=8, t=PACK)[:, :, 0, :],
        )
        load_kq(1)
        load_v(0)
        behind = []
        for s in range(H + 2):
            if s + 2 < H:
                load_kq(s + 2)
            if s + 1 < H:
                load_v(s + 1)
            if 1 <= s < 4:
                load_w(*w_units[s])
            if s == 4:
                nc.sync.dma_start(out=bias[:], in_=bo.partition_broadcast(P))
            r_done = [hg for hg in range(2) if s == HG * hg + HG + 1]
            r_ready = [hg for hg in range(2) if s == HG * hg + HG + 2]

            if s < H and s != 1:
                turn_keys(s)
            for hg in r_ready:
                r_exps(hg)
            if 1 <= s <= H:
                scores(s - 1)
            if s == 1:
                turn_keys(s)
            if s >= 2:
                exps(s - 2)
            if s < H:
                turn_queries(s)
            if s >= 2:
                r_scores(s - 2)
            if s == HG + 3:
                r_turn(0)
            if 1 <= s <= H:
                v_regroup(s - 1)
            if s == H + 0:
                w_regroup_on_scalar(*w_units[3])
            if s == HG + 5:
                r_attend(0)

            fillers, behind = behind, []
            if s == 1:
                fillers += [make_mask_r] + [make_diag] + [open_mask_r]
                fillers += [make_ident32, make_head_of, va_regroup, make_own_head] + va_spread()
                behind += [va_quantise]
            if s == 2:
                fillers += [lambda: nc.vector.memset(e_pad[:, :, H * NB : PACK * P].bitcast(I32), 0)]
            if s >= 2:
                fillers = [lambda h=s - 2: v_quantise(h)] + fillers
            if 3 <= s < N_EARLY + 3:
                fillers += head_fills(s - 3)
                behind += [lambda h=s - 3: head_quantise(h)]
            if s in W_STEPS:
                unit = w_units[W_STEPS.index(s)]
                fillers += [lambda u=unit: w_regroup(*u)]
                behind += [lambda u=unit: w_quantise(*u)]
            if s == HG + 3:
                fillers += [lambda: r_sum(0)]
            if s == HG + 4:
                fillers += [lambda: r_inverse(0), lambda: r_quantise(0)]
            if s == HG + 5:
                fillers += [lambda: r_factors(0)]
            chain = []
            for hg in r_done:
                chain += [lambda: r_highs(hg), lambda: r_top(hg), lambda: r_shift(hg)]
            if 1 <= s <= H:
                chain += [lambda: find_highs(s - 1), lambda: find_top(s - 1), lambda: find_shifts(s - 1)]
            weave(chain, fillers, len(fillers) if s == 1 else len(fillers) // 4)

        order = [1, 2, 3, 4, 5, 0, 6, 7]
        fills = tile_fills(order[0])
        for j0 in range(0, NT, 2):
            turn_a(j0)
        for f in behind:
            f()
        nc.vector.tensor_tensor(out=rsum[:], in0=rsum_a[:], in1=e_own[:], op=ALU.add)
        for f in fills:
            f()
        nc.vector.reciprocal(out=rinv[:], in_=rsum[:])
        quantise_a(0)
        tile_quantise(order[0])
        for j0 in range(2, NT, 2):
            quantise_a(j0)
        w_quantise(*w_units[3])
        for i in range(NT + 2):
            if i < NT:
                attend(order[i], i == NT - 1)
            if 1 <= i <= NT:
                turn_ctx(order[i - 1])
            if i == 3:
                r_turn_ctx(0)
            if i == 5:
                r_turn_ctx(1)
            if i >= 2:
                project(order[i - 2], i == NT + 1)
            if i == 0:
                r_exps(1)
            if i == 1:
                r_turn(1)
            if i == 3:
                r_attend(1)
            if i + 1 < NT:
                for f in tile_fills(order[i + 1]):
                    f()
            if i == 1:
                r_sum(1)
            if i == 2:
                r_inverse(1)
                r_quantise(1)
                r_pick(0)
            if i == 3:
                r_factors(1)
            if i == 4:
                r_pick(1)
            if 3 <= i <= NT:
                add_bias(order[i - 3], 1)
                store(order[i - 3], 1)
            if i + 1 < NT:
                tile_quantise(order[i + 1])
            if i == 2:
                r_join(0)
            if i == 4:
                r_join(1)
            if 1 <= i <= NT:
                quantise_ctx(order[i - 1])
            if i >= 2:
                add_bias(order[i - 2], 0)
                store(order[i - 2], 0)
            if i >= NT:
                add_bias(order[i - 2], 1)
                store(order[i - 2], 1)
